import numpy as np
import ml_dtypes


def mxq(x, axis, fmt="e4m3"):
    dtype, down = {"e4m3": (ml_dtypes.float8_e4m3fn, 7), "e5m2": (ml_dtypes.float8_e5m2, 14)}[fmt]
    v = np.moveaxis(np.asarray(x, np.float32).astype(ml_dtypes.bfloat16).astype(np.float64), axis, -1)
    blocks = v.reshape(v.shape[:-1] + (-1, 32))
    amax = np.abs(blocks).max(-1, keepdims=True)
    byte = np.maximum(np.where(amax > 0, np.frexp(amax)[1] - 1 + 127, 0) - down, 1)
    scale = np.exp2(byte - 127.0)
    codes = (blocks / scale).astype(np.float32).astype(dtype).astype(np.float64)
    return np.moveaxis((codes * scale).reshape(v.shape), -1, axis)


WIDE = False


def mx_kscale(k):
    if not WIDE:
        return np.ones(k)
    levels = np.array([10, -10, 5, -5, 0])
    if k % 512:
        return np.exp2(np.random.permutation(np.resize(levels, k // 32))).repeat(32)
    a = np.empty((k // 512, 16))
    for p in range(k // 512):
        a[p, :8] = np.random.permutation(np.resize(levels, 8))
        for g in range(8):
            far = levels[np.abs(levels - a[p, g]) >= 10]
            a[p, g + 8] = far[np.random.randint(len(far))]
    return np.exp2(a.ravel()).repeat(32)


BF16 = ml_dtypes.bfloat16


def bf(x):
    return np.asarray(x, np.float32).astype(BF16)


def f64(x):
    return np.asarray(x).astype(np.float64)


B, S, M, H, KV, HD = 2, 256, 2048, 16, 4, 128
ROT = HD // 4
HALF = ROT // 2
EPS = 1e-6
MAX_WAVELENGTH = 10000.0


def rms_norm(x, scale):
    var = np.mean(np.square(x), axis=-1, keepdims=True)
    return x * (1.0 / np.sqrt(var + EPS)) * scale


def partial_rope(x):
    x_rope, x_pass = x[..., :ROT], x[..., ROT:]
    pos = np.arange(S, dtype=np.float64)
    inv_freq = 1.0 / (MAX_WAVELENGTH ** (np.arange(0, ROT, 2, dtype=np.float64) / ROT))
    freq = pos[:, None] * inv_freq[None, :]
    emb = np.concatenate([freq, freq], axis=-1)
    cos = np.cos(emb)[None, :, None, :]
    sin = np.sin(emb)[None, :, None, :]
    x1, x2 = x_rope[..., :HALF], x_rope[..., HALF:]
    rotated = np.concatenate([-x2, x1], axis=-1)
    x_rope = x_rope * cos + rotated * sin
    return np.concatenate([x_rope, x_pass], axis=-1)


def draw0():
    s = mx_kscale(M)
    w = 1.0 / np.sqrt(M) / s[:, None, None]
    return {"hidden_states": bf(np.random.standard_normal((B, S, M)) * s),
            "Wq_query": bf(np.random.standard_normal((M, H, HD)) * w),
            "Wk": bf(np.random.standard_normal((M, KV, HD)) * w),
            "Wv": bf(np.random.standard_normal((M, KV, HD)) * 2.0 * w),
            "q_scale": bf(1.0 + 0.1 * np.random.standard_normal(HD)),
            "k_scale": bf(1.0 + 0.1 * np.random.standard_normal(HD))}


def core(hidden_states, Wq_query, Wk, Wv, q_scale, k_scale):
    xq = mxq(f64(hidden_states).reshape(B * S, M), 1, "e4m3")
    query = (xq @ mxq(f64(Wq_query).reshape(M, H * HD), 0, "e4m3")).reshape(B, S, H, HD)
    key = (xq @ mxq(f64(Wk).reshape(M, KV * HD), 0, "e4m3")).reshape(B, S, KV, HD)
    value = (xq @ mxq(f64(Wv).reshape(M, KV * HD), 0, "e4m3")).reshape(B, S, KV, HD)
    query = partial_rope(rms_norm(query, f64(q_scale)))
    key = partial_rope(rms_norm(key, f64(k_scale)))
    return query, key, value


def e4m3fn_bytes(y):
    return np.clip(np.asarray(y, np.float64), -448.0, 448.0).astype(np.float32).astype(ml_dtypes.float8_e4m3fn).view(np.uint8)


def e4m3fn_values(b):
    return np.asarray(b, np.uint8).view(ml_dtypes.float8_e4m3fn).astype(np.float64)


def setup_inputs():
    d = draw0()
    x0 = np.asarray(d['Wq_query']).astype(np.float64)
    s = (np.max(np.abs(x0), axis=(1, 2), keepdims=True) / 448.0).astype(np.float32)
    out = {}
    for k, v in d.items():
        if k == 'Wq_query':
            out['Wq_query_bytes'] = e4m3fn_bytes(x0 / s.astype(np.float64))
            out['Wq_query_scale'] = s
        else:
            out[k] = v
    return out


def reference(hidden_states, Wq_query_bytes, Wq_query_scale, Wk, Wv, q_scale, k_scale):
    return core(hidden_states, e4m3fn_values(Wq_query_bytes) * Wq_query_scale.astype(np.float64), Wk, Wv, q_scale, k_scale)

@@ -1,0 +1,405 @@
+from contextlib import ExitStack
+import math
+
+import concourse.mybir as mybir
+from concourse.masks import make_identity
+
+F32 = mybir.dt.float32
+BF16 = mybir.dt.bfloat16
+I32 = mybir.dt.int32
+U32 = mybir.dt.uint32
+U8 = mybir.dt.uint8
+FP8 = mybir.dt.float8_e4m3fn
+FP8X4 = mybir.dt.float8_e4m3fn_x4
+ACT = mybir.ActivationFunctionType
+ALU = mybir.AluOpType
+
+P = 128
+TOKENS = 512
+FEATURES = 2048
+PASSES = 4
+TT = 4
+CW = 512
+HD = 128
+HEADS = 4
+EPS = 1e-6
+FLOPS = 2 * TOKENS * FEATURES * 3072
+
+KCH, VCH = 0, 5
+S_INTERLEAVES = ((5, 0), (5, 1), (5, 2), (5, 3))
+V_AT = [14, 18, 22, 23]
+WIDE_BUFS = 4
+GROUPED_BUFS = 4
+OUT_BUFS = 8
+WV_LOAD_AFTER = 1
+LOOK = 2
+D_SQ = 3
+D_NORM = 4
+RATE = 2
+
+
+def tile_qwen3_5attention_pa_kernel(
+    tc, hidden_states, Wq_query_bytes, Wq_query_scale, Wk, Wv, q_scale, k_scale, out_0, out_1, out_2
+):
+    nc = tc.nc
+    x_dram = hidden_states.flatten_outer_dims().rearrange("(a p) k -> a p k", p=P)
+    wq_dram = Wq_query_bytes.rearrange("(g p t) u h -> g p t (u h)", p=P, t=4)
+    wqs_dram = Wq_query_scale.rearrange("(g p t) a b -> p g (t a b)", p=P, t=4)
+    wk_dram = Wk.rearrange("(g p t) u h -> g p t (u h)", p=P, t=4)
+    wv_dram = Wv.rearrange("(g p t) u h -> g p t (u h)", p=P, t=4)
+    outq_dram = out_0.rearrange("b s u h -> (b s) (u h)").rearrange("(a p) c -> a p c", p=P)
+    outk_dram = out_1.rearrange("b s u h -> (b s) (u h)").rearrange("(a p) c -> a p c", p=P)
+    outv_dram = out_2.rearrange("b s u h -> (b s) (u h)").rearrange("(a p) c -> a p c", p=P)
+
+    with ExitStack() as ctx:
+        keep = ctx.enter_context(tc.tile_pool(name="keep", bufs=1))
+        stage = ctx.enter_context(tc.tile_pool(name="stage", bufs=2))
+        psum = ctx.enter_context(tc.psum_pool(name="psum", bufs=1))
+        ctx.enter_context(tc.manual_schedule())
+
+        x_sb = keep.tile([P, TT, FEATURES], BF16, name="x_sb")
+        wq_bytes = keep.tile([P, 4, PASSES, 4, CW], U8, name="wq_bytes")
+        wq_scale = keep.tile([P, PASSES, 4], F32, name="wq_scale")
+        wk_sb = keep.tile([P, PASSES, 4, CW], BF16, name="wk_sb")
+        wv_sb = keep.tile([P, PASSES, 4, CW], BF16, name="wv_sb")
+        w_codes = keep.tile([P, 6, PASSES, CW], U32, name="w_codes", align_bytes=64)
+        w_scales = keep.tile([P, 6, PASSES, CW], U8, name="w_scales", align_bytes=64)
+        x_codes = keep.tile([P, TT, PASSES, P], U32, name="x_codes", align_bytes=64)
+        x_scales = keep.tile([P, TT, PASSES, P], U8, name="x_scales", align_bytes=64)
+        ident = keep.tile([P, P], F32, name="ident")
+        ones = keep.tile([P, P], BF16, name="ones")
+        gain_rows = keep.tile([P, 2 * HD], BF16, name="gain_rows")
+        pos_i = keep.tile([P, 4, 16], I32, name="pos_i")
+        quarter_i = keep.tile([P, 4, 16], I32, name="quarter_i")
+        tau = keep.tile([P, 16], F32, name="tau")
+        one = keep.tile([P, 1], F32, name="one")
+        turns = keep.tile([P, 4, 16], F32, name="turns")
+        turns2 = keep.tile([P, 4, 16], F32, name="turns2")
+        whole_i = keep.tile([P, 4, 16], I32, name="whole_i")
+        frac = keep.tile([P, 4, 16], F32, name="frac")
+        wrapped = keep.tile([P, 4, 16], F32, name="wrapped")
+        trig = keep.tile([P, 2, 4, 16], F32, name="trig")
+        warm = keep.tile([P, 1], F32, name="warm")
+        gain_cos = keep.tile([P, 2, 2, HD], F32, name="gain_cos")
+        gain_sin = keep.tile([P, 2, 2, 32], F32, name="gain_sin")
+
+        def bank(b):
+            return psum.tile([P, CW], F32, name="bank%d" % b, tag="bank%d" % b)
+
+        def load_wq(c, g):
+            nc.sync.dma_start(out=wq_bytes[:, c, g, :, :], in_=wq_dram[g][:, :, c * CW : (c + 1) * CW])
+
+        nc.scalar.dma_start(out=wq_scale[:], in_=wqs_dram)
+        nc.gpsimd.memset(gain_rows[:], 0.0)
+        nc.gpsimd.iota(pos_i[:].rearrange("p (j b) i -> p j b i", j=2), pattern=[[P, 2], [0, 2], [0, 16]], base=0, channel_multiplier=1)
+        nc.gpsimd.iota(quarter_i[:].rearrange("p (j b) i -> p j b i", j=2), pattern=[[0, 2], [1, 2], [0, 16]], base=0, channel_multiplier=0)
+        nc.scalar.dma_start(out=gain_rows[0:1, 0:HD], in_=q_scale.unsqueeze(0))
+        nc.scalar.dma_start(out=gain_rows[0:1, HD : 2 * HD], in_=k_scale.unsqueeze(0))
+        nc.gpsimd.memset(ones[:], 1.0)
+        make_identity(nc, ident[:])
+        for s in range(PASSES):
+            nc.sync.dma_start(out=wk_sb[:, s], in_=wk_dram[s])
+            load_wq(0, s)
+            nc.sync.dma_start(out=x_sb[:, s, :], in_=x_dram[s])
+        for c in range(1, 4):
+            for g in range(PASSES):
+                load_wq(c, g)
+            if c == WV_LOAD_AFTER:
+                for g in range(PASSES):
+                    nc.sync.dma_start(out=wv_sb[:, g], in_=wv_dram[g])
+
+        ratio = 10000.0 ** (-1.0 / 16.0)
+        nc.vector.memset(one[:], 1.0)
+        nc.vector.tensor_scalar(out=tau[:, 0:1], in0=one[:], scalar1=1.0 / (2.0 * math.pi), scalar2=None, op0=ALU.mult)
+        for w in (1, 2, 4, 8):
+            nc.vector.tensor_scalar(out=tau[:, w : 2 * w], in0=tau[:, 0:w], scalar1=ratio**w, scalar2=None, op0=ALU.mult)
+        nc.vector.tensor_tensor(out=turns[:], in0=pos_i[:], in1=tau[:].unsqueeze(1).to_broadcast([P, 4, 16]), op=ALU.mult)
+        nc.vector.scalar_tensor_tensor(out=turns2[:], in0=quarter_i[:], scalar=0.25, in1=turns[:], op0=ALU.mult, op1=ALU.add)
+        nc.vector.tensor_copy(out=whole_i[:], in_=turns2[:])
+        nc.vector.scalar_tensor_tensor(out=frac[:], in0=whole_i[:], scalar=-1.0, in1=turns2[:], op0=ALU.mult, op1=ALU.add)
+        nc.vector.scalar_tensor_tensor(out=wrapped[:], in0=frac[:], scalar=0.5, in1=frac[:], op0=ALU.is_gt, op1=ALU.subtract)
+        nc.scalar.activation(
+            out=trig[:, :, 0:2, :], in_=wrapped[:].rearrange("p (j b) i -> p j b i", j=2), func=ACT.Sin, scale=-2.0 * math.pi
+        )
+        nc.scalar.activation(out=warm[:], in_=one[:], func=ACT.Sqrt)
+        nc.gpsimd.tensor_scalar(out=trig[:, :, 2, :], in0=trig[:, :, 0, :], scalar1=-1.0, scalar2=0.0, op0=ALU.mult, op1=ALU.add)
+
+        wides = {}
+        groupeds = {}
+        banks = {}
+        x_groupeds = {}
+        stats = {}
+
+        def widen(ci, g, between):
+            wide = stage.tile([P, 4, CW], BF16, name="wide", bufs=WIDE_BUFS)
+            for t in range(4):
+                nc.scalar.activation(
+                    out=wide[:, t, :], in_=wq_bytes[:, ci - 1, g, t, :].bitcast(FP8), func=ACT.Copy, scale=wq_scale[:, g, t : t + 1]
+                )
+                if t == 0:
+                    between()
+            wides[(ci, g)] = wide
+
+        def interleave(ci, g):
+            src = wk_sb[:, g] if ci == KCH else wv_sb[:, g] if ci == VCH else wides[(ci, g)]
+            if (ci, g) in S_INTERLEAVES:
+                grouped = stage.tile([P, 4 * CW], BF16, name="grouped_s", bufs=2, align_bytes=64)
+                nc.scalar.copy(out=grouped.rearrange("p (n t) -> p n t", t=4), in_=src.rearrange("p t n -> p n t"))
+            else:
+                grouped = stage.tile([P, 4 * CW], BF16, name="grouped", bufs=GROUPED_BUFS, align_bytes=64)
+                nc.vector.tensor_copy(out=grouped.rearrange("p (n t) -> p n t", t=4), in_=src.rearrange("p t n -> p n t"))
+            groupeds[(ci, g)] = grouped
+
+        def quantize(ci, g):
+            nc.vector.quantize_mx(out=w_codes[:, ci, g, :].bitcast(FP8X4), scales=w_scales[:, ci, g, :], in_=groupeds[(ci, g)][:, :])
+
+        def multiply(ci, g, a):
+            nc.tensor.matmul_mx(
+                out=banks[(ci, a)][:, :],
+                lhsT=x_codes[:, a, g, :].bitcast(FP8X4),
+                lhsT_scale=x_scales[:, a, g, :],
+                rhs=w_codes[:, ci, g, :].bitcast(FP8X4),
+                rhs_scale=w_scales[:, ci, g, :],
+                start=(g == 0),
+                stop=(g == PASSES - 1),
+            )
+
+        def x_transpose(a):
+            words = x_sb[:, a, :].bitcast(F32)
+            xg = stage.tile([P, PASSES, P, 4], BF16, name="x_grouped", bufs=2, align_bytes=64)
+            x_groupeds[a] = xg
+            for half in range(2):
+                xt = bank(a + 4 * half)
+                xt4 = xt.rearrange("p (c r) -> p c r", c=4)
+                for c in range(4):
+                    g, u = 2 * half + c // 2, c % 2
+                    nc.tensor.transpose(xt4[:, c, :], words[:, 256 * g + u : 256 * (g + 1) : 2], ident[:])
+                banks[("x", a, half)] = xt
+
+        def x_copy(a):
+            xg = x_groupeds[a]
+            for half in range(2):
+                nc.scalar.copy(
+                    out=xg[:, 2 * half : 2 * half + 2].rearrange("p g r t -> p g (r t)").bitcast(F32).rearrange("p g (r u) -> p g r u", u=2),
+                    in_=banks[("x", a, half)].rearrange("p (g u r) -> p g r u", g=2, u=2),
+                )
+
+        def x_quantize(a):
+            nc.vector.quantize_mx(
+                out=x_codes[:, a].rearrange("p g r -> p (g r)").bitcast(FP8X4),
+                scales=x_scales[:, a].rearrange("p g r -> p (g r)"),
+                in_=x_groupeds[a].rearrange("p g r t -> p (g r t)"),
+            )
+
+        def store(ci, a, o):
+            if ci == KCH:
+                dst = outk_dram[a]
+            elif ci == VCH:
+                dst = outv_dram[a]
+            else:
+                dst = outq_dram[a][:, (ci - 1) * CW : ci * CW]
+            nc.sync.dma_start(out=dst, in_=o[:, :])
+
+        def squares(ci, a):
+            ss = stage.tile([P, HEADS], F32, name="ss", bufs=4)
+            for h in range(HEADS):
+                junk = stage.tile([P, HD], F32, name="junk", bufs=2)
+                nc.scalar.activation(out=junk[:], in_=banks[(ci, a)][:, h * HD : (h + 1) * HD], func=ACT.Square, accum_out=ss[:, h : h + 1])
+            stats[(ci, a)] = ss
+
+        def root(ci, a):
+            rms = stage.tile([P, HEADS], F32, name="rms", bufs=4)
+            nc.scalar.activation(out=rms[:], in_=stats[(ci, a)][:], func=ACT.Sqrt, scale=1.0 / HD, bias=EPS)
+            stats[(ci, a)] = rms
+
+        def norm_a(ci, a):
+            rstd = stage.tile([P, HEADS], F32, name="rstd", bufs=4)
+            nc.vector.reciprocal(out=rstd[:], in_=stats[(ci, a)][:])
+            stats[(ci, a)] = rstd
+
+        def norm_b(ci, a):
+            qk = 1 if ci == KCH else 0
+            rstd = stats[(ci, a)]
+            o = stage.tile([P, CW], F32, name="o", bufs=OUT_BUFS)
+            ysin = stage.tile([P, HEADS, 32], F32, name="ysin", bufs=4)
+            acc = banks[(ci, a)]
+            for h in range(HEADS):
+                nc.vector.scalar_tensor_tensor(
+                    out=o[:, h * HD : (h + 1) * HD],
+                    in0=acc[:, h * HD : (h + 1) * HD],
+                    scalar=rstd[:, h : h + 1],
+                    in1=gain_cos[:, qk, a % 2, :],
+                    op0=ALU.mult,
+                    op1=ALU.mult,
+                )
+                nc.vector.scalar_tensor_tensor(
+                    out=ysin[:, h, :],
+                    in0=acc[:, h * HD : h * HD + 32],
+                    scalar=rstd[:, h : h + 1],
+                    in1=gain_sin[:, qk, a % 2, :],
+                    op0=ALU.mult,
+                    op1=ALU.mult,
+                )
+            stats[(ci, a)] = (o, ysin)
+
+        def norm_c(ci, a, half):
+            o, ysin = stats[(ci, a)]
+            oh = o.rearrange("p (h d) -> p h d", h=HEADS)
+            lo, hi = 16 * half, 16 * half + 16
+            nc.vector.tensor_tensor(out=oh[:, :, lo:hi], in0=oh[:, :, lo:hi], in1=ysin[:, :, 16 - lo : 32 - lo], op=ALU.add)
+            if half == 1:
+                store(ci, a, o)
+
+        def value_out(a):
+            o = stage.tile([P, CW], F32, name="o", bufs=OUT_BUFS)
+            if a % 2 == 0:
+                nc.scalar.copy(out=o[:, :], in_=banks[(VCH, a)][:, :])
+            else:
+                nc.vector.tensor_copy(out=o[:, :], in_=banks[(VCH, a)][:, :])
+            store(VCH, a, o)
+
+        def gain_matmul():
+            gb = bank(7)
+            nc.tensor.matmul(out=gb[:, 0 : 2 * HD], lhsT=ones[:], rhs=gain_rows[:], start=True, stop=True)
+            banks["gains"] = gb
+
+        def gain_tables():
+            gb = banks["gains"]
+            for j in range(2):
+                nc.vector.tensor_copy(out=gain_cos[:, :, j, :], in_=gb[:, 0 : 2 * HD].rearrange("p (q d) -> p q d", q=2))
+            for j in range(2):
+                first = gain_cos[:, :, j, 0:32].rearrange("p q (h i) -> p q h i", h=2)
+                nc.gpsimd.tensor_tensor(
+                    out=gain_sin[:, :, j, :].rearrange("p q (h i) -> p q h i", h=2),
+                    in0=first,
+                    in1=trig[:, j, 0:3:2, :].unsqueeze(1).to_broadcast([P, 2, 2, 16]),
+                    op=ALU.mult,
+                )
+                nc.gpsimd.tensor_tensor(
+                    out=first, in0=first, in1=trig[:, j, 1:2, :].unsqueeze(1).to_broadcast([P, 2, 2, 16]), op=ALU.mult
+                )
+
+        units = []
+        for s in range(PASSES):
+            units.extend([(KCH, s), (1, s)])
+        units.extend([(ci, g) for ci in range(2, 5) for g in range(PASSES)])
+        others = list(units)
+        units.clear()
+        for i in range(len(others) + PASSES):
+            if i in V_AT:
+                units.append((VCH, V_AT.index(i)))
+            else:
+                units.append(others[i - len([v for v in V_AT if v < i])])
+        n = len(units)
+        last_step = {}
+        for i in range(n):
+            last_step[units[i][0]] = i
+        bank_of = {0: 0, 1: 4, 2: 0, 3: 4, 4: 0, 5: 4}
+        bank_user = {}
+        turns_done = {}
+        pending = []
+        x_ready = []
+        sq_todo = [(ci, a) for ci in range(5) for a in range(TT)]
+        norm_todo = [(ci, a) for ci in range(6) for a in range(TT)]
+        sq_done = []
+        mm_left = {}
+        for ci in range(6):
+            for a in range(TT):
+                mm_left[(ci, a)] = PASSES
+
+        roots = []
+
+        def do_roots():
+            for item in roots:
+                root(item[0], item[1])
+                sq_done.append(item)
+            roots.clear()
+
+        def first_stage(i):
+            if i < n:
+                ci, g = units[i]
+                if ci not in (KCH, VCH):
+                    widen(ci, g, do_roots)
+                elif (ci, g) in S_INTERLEAVES:
+                    interleave(ci, g)
+            do_roots()
+
+        def second_stage(i):
+            if i < n and units[i] not in S_INTERLEAVES:
+                interleave(units[i][0], units[i][1])
+
+        def run_matmuls():
+            for item in list(pending):
+                ci, g, a = item
+                b = bank_of[ci] + a
+                if a not in x_ready:
+                    continue
+                if (ci, a) not in banks:
+                    if bank_user.get(b) is not None or turns_done.get(b, 0) != ci // 2:
+                        continue
+                    banks[(ci, a)] = bank(b)
+                    bank_user[b] = (ci, a)
+                if any(p[0] == ci and p[2] == a and p[1] < g for p in pending):
+                    continue
+                multiply(ci, g, a)
+                mm_left[(ci, a)] -= 1
+                pending.remove(item)
+
+        def take_x(a):
+            for half in range(2):
+                assert bank_user.get(a + 4 * half) is None
+            x_transpose(a)
+
+        gain_matmul()
+        for i in range(LOOK):
+            first_stage(i)
+        take_x(0)
+        second_stage(0)
+        def take(todo):
+            item = todo[0]
+            todo.remove(item)
+            return item
+
+        for i in range(n + 12):
+            k = 0
+            while sq_todo and k < RATE and mm_left[sq_todo[0]] == 0 and i >= last_step[sq_todo[0][0]] + D_SQ:
+                squares(sq_todo[0][0], sq_todo[0][1])
+                roots.append(take(sq_todo))
+                k += 1
+            first_stage(i + LOOK)
+            if i % 2 == 0 and i // 2 < TT:
+                a = i // 2
+                if a + 1 < TT:
+                    if a + 1 == 3:
+                        gain_tables()
+                    take_x(a + 1)
+                x_copy(a)
+            now = []
+            while norm_todo and len(now) < RATE and mm_left[norm_todo[0]] == 0 and i >= last_step[norm_todo[0][0]] + D_NORM:
+                if norm_todo[0][0] != VCH and norm_todo[0] not in sq_done:
+                    break
+                now.append(take(norm_todo))
+            for ci, a in now:
+                if ci != VCH:
+                    norm_a(ci, a)
+            second_stage(i + 1)
+            for ci, a in now:
+                if ci == VCH:
+                    value_out(a)
+                else:
+                    norm_b(ci, a)
+                bank_user[bank_of[ci] + a] = None
+                turns_done[bank_of[ci] + a] = ci // 2 + 1
+            if i < n:
+                quantize(units[i][0], units[i][1])
+                for a in range(TT):
+                    pending.append((units[i][0], units[i][1], a))
+            if i % 2 == 1 and i // 2 < TT:
+                x_quantize(i // 2)
+                x_ready.append(i // 2)
+            for half in range(2):
+                for ci, a in now:
+                    if ci != VCH:
+                        norm_c(ci, a, half)
+            run_matmuls()
+        assert not pending and not norm_todo and not sq_todo

@@ -26,8 +26,12 @@ EPS = 1e-6
 FLOPS = 2 * TOKENS * FEATURES * 3072
 
 KCH, VCH = 0, 5
-S_INTERLEAVES = ((5, 0), (5, 1), (5, 2), (5, 3))
+G_ASSIST = True
+S_INTERLEAVES = [(4, 3)]
 V_AT = [14, 18, 22, 23]
+HEAD = [(0, 0), (0, 1), (1, 0), (0, 2), (1, 1), (0, 3), (1, 2), (1, 3)]
+LOADS = ["k0", "q0", "k1", "q1", "x0", "k2", "q2", "x1", "k3", "q3", "x2", "x3"]
+X_AFTER = [2, 4, 5, 6]
 WIDE_BUFS = 4
 GROUPED_BUFS = 4
 OUT_BUFS = 8
@@ -97,10 +101,14 @@ def tile_qwen3_5attention_pa_kernel(
         nc.scalar.dma_start(out=gain_rows[0:1, HD : 2 * HD], in_=k_scale.unsqueeze(0))
         nc.gpsimd.memset(ones[:], 1.0)
         make_identity(nc, ident[:])
-        for s in range(PASSES):
-            nc.sync.dma_start(out=wk_sb[:, s], in_=wk_dram[s])
-            load_wq(0, s)
-            nc.sync.dma_start(out=x_sb[:, s, :], in_=x_dram[s])
+        for what in LOADS:
+            s = int(what[1])
+            if what[0] == "k":
+                nc.sync.dma_start(out=wk_sb[:, s], in_=wk_dram[s])
+            elif what[0] == "q":
+                load_wq(0, s)
+            else:
+                nc.sync.dma_start(out=x_sb[:, s, :], in_=x_dram[s])
         for c in range(1, 4):
             for g in range(PASSES):
                 load_wq(c, g)
@@ -166,8 +174,6 @@ def tile_qwen3_5attention_pa_kernel(
 
         def x_transpose(a):
             words = x_sb[:, a, :].bitcast(F32)
-            xg = stage.tile([P, PASSES, P, 4], BF16, name="x_grouped", bufs=2, align_bytes=64)
-            x_groupeds[a] = xg
             for half in range(2):
                 xt = bank(a + 4 * half)
                 xt4 = xt.rearrange("p (c r) -> p c r", c=4)
@@ -177,7 +183,8 @@ def tile_qwen3_5attention_pa_kernel(
                 banks[("x", a, half)] = xt
 
         def x_copy(a):
-            xg = x_groupeds[a]
+            xg = stage.tile([P, PASSES, P, 4], BF16, name="x_grouped", bufs=2, align_bytes=64)
+            x_groupeds[a] = xg
             for half in range(2):
                 nc.scalar.copy(
                     out=xg[:, 2 * half : 2 * half + 2].rearrange("p g r t -> p g (r t)").bitcast(F32).rearrange("p g (r u) -> p g r u", u=2),
@@ -258,6 +265,29 @@ def tile_qwen3_5attention_pa_kernel(
                 nc.vector.tensor_copy(out=o[:, :], in_=banks[(VCH, a)][:, :])
             store(VCH, a, o)
 
+        def g_interleave(k):
+            g, half = k // 2, k % 2
+            grouped = stage.tile([P, 2 * CW], BF16, name="grouped_g", bufs=1, align_bytes=64)
+            if k == 0:
+                nc.vector.memset(grouped[:, 0:2], 1.0)
+            nc.gpsimd.tensor_scalar(
+                out=grouped.rearrange("p (n t) -> p n t", t=4),
+                in0=wv_sb[:, g, :, half * 256 : half * 256 + 256].rearrange("p t n -> p n t"),
+                scalar1=1.0,
+                scalar2=0.0,
+                op0=ALU.mult,
+                op1=ALU.add,
+            )
+            groupeds[("g", k)] = grouped
+
+        def g_quantize(k):
+            g, half = k // 2, k % 2
+            cols = slice(half * 256, half * 256 + 256)
+            nc.vector.quantize_mx(out=w_codes[:, VCH, g, cols].bitcast(FP8X4), scales=w_scales[:, VCH, g, cols], in_=groupeds[("g", k)][:, :])
+            if half == 1:
+                for a in range(TT):
+                    pending.append((VCH, g, a))
+
         def gain_matmul():
             gb = bank(7)
             nc.tensor.matmul(out=gb[:, 0 : 2 * HD], lhsT=ones[:], rhs=gain_rows[:], start=True, stop=True)
@@ -279,21 +309,23 @@ def tile_qwen3_5attention_pa_kernel(
                     out=first, in0=first, in1=trig[:, j, 1:2, :].unsqueeze(1).to_broadcast([P, 2, 2, 16]), op=ALU.mult
                 )
 
-        units = []
-        for s in range(PASSES):
-            units.extend([(KCH, s), (1, s)])
+        units = list(HEAD)
         units.extend([(ci, g) for ci in range(2, 5) for g in range(PASSES)])
-        others = list(units)
-        units.clear()
-        for i in range(len(others) + PASSES):
-            if i in V_AT:
-                units.append((VCH, V_AT.index(i)))
-            else:
-                units.append(others[i - len([v for v in V_AT if v < i])])
+        if not G_ASSIST:
+            others = list(units)
+            units.clear()
+            for i in range(len(others) + PASSES):
+                if i in V_AT:
+                    units.append((VCH, V_AT.index(i)))
+                else:
+                    units.append(others[i - len([v for v in V_AT if v < i])])
         n = len(units)
         last_step = {}
         for i in range(n):
             last_step[units[i][0]] = i
+        if G_ASSIST:
+            last_step[VCH] = 0
+        windows = [0]
         bank_of = {0: 0, 1: 4, 2: 0, 3: 4, 4: 0, 5: 4}
         bank_user = {}
         turns_done = {}
@@ -320,7 +352,7 @@ def tile_qwen3_5attention_pa_kernel(
                 ci, g = units[i]
                 if ci not in (KCH, VCH):
                     widen(ci, g, do_roots)
-                elif (ci, g) in S_INTERLEAVES:
+                if (ci, g) in S_INTERLEAVES:
                     interleave(ci, g)
             do_roots()
 
@@ -367,8 +399,8 @@ def tile_qwen3_5attention_pa_kernel(
                 roots.append(take(sq_todo))
                 k += 1
             first_stage(i + LOOK)
-            if i % 2 == 0 and i // 2 < TT:
-                a = i // 2
+            if i in X_AFTER:
+                a = X_AFTER.index(i)
                 if a + 1 < TT:
                     if a + 1 == 3:
                         gain_tables()
@@ -383,6 +415,15 @@ def tile_qwen3_5attention_pa_kernel(
                 if ci != VCH:
                     norm_a(ci, a)
             second_stage(i + 1)
+            if G_ASSIST and windows[0] == 2 * PASSES:
+                g_quantize(2 * PASSES - 1)
+                windows[0] += 1
+            if G_ASSIST and now and now[0][0] != VCH:
+                if 0 < windows[0] < 2 * PASSES:
+                    g_quantize(windows[0] - 1)
+                if windows[0] < 2 * PASSES:
+                    g_interleave(windows[0])
+                    windows[0] += 1
             for ci, a in now:
                 if ci == VCH:
                     value_out(a)
@@ -394,9 +435,9 @@ def tile_qwen3_5attention_pa_kernel(
                 quantize(units[i][0], units[i][1])
                 for a in range(TT):
                     pending.append((units[i][0], units[i][1], a))
-            if i % 2 == 1 and i // 2 < TT:
-                x_quantize(i // 2)
-                x_ready.append(i // 2)
+            if i - 1 in X_AFTER:
+                x_quantize(X_AFTER.index(i - 1))
+                x_ready.append(X_AFTER.index(i - 1))
             for half in range(2):
                 for ci, a in now:
                     if ci != VCH:

@@ -152,10 +152,10 @@ def tile_qwen3_5attention_pa_kernel(
             src = wk_sb[:, g] if ci == KCH else wv_sb[:, g] if ci == VCH else wides[(ci, g)]
             if (ci, g) in S_INTERLEAVES:
                 grouped = stage.tile([P, 4 * CW], BF16, name="grouped_s", bufs=2, align_bytes=64)
-                nc.scalar.copy(out=grouped.rearrange("p (n t) -> p n t", t=4), in_=src.rearrange("p t n -> p n t"))
+                nc.scalar.copy(out=grouped.rearrange("p (c i t) -> p c t i", i=4, t=4), in_=src.rearrange("p t (c i) -> p c t i", i=4))
             else:
                 grouped = stage.tile([P, 4 * CW], BF16, name="grouped", bufs=GROUPED_BUFS, align_bytes=64)
-                nc.vector.tensor_copy(out=grouped.rearrange("p (n t) -> p n t", t=4), in_=src.rearrange("p t n -> p n t"))
+                nc.vector.tensor_copy(out=grouped.rearrange("p (c i t) -> p c t i", i=4, t=4), in_=src.rearrange("p t (c i) -> p c t i", i=4))
             groupeds[(ci, g)] = grouped
 
         def quantize(ci, g):
@@ -259,7 +259,7 @@ def tile_qwen3_5attention_pa_kernel(
 
         def value_out(a):
             o = stage.tile([P, CW], F32, name="o", bufs=OUT_BUFS)
-            if a % 2 == 0:
+            if a % 2 == 0 or G_ASSIST:
                 nc.scalar.copy(out=o[:, :], in_=banks[(VCH, a)][:, :])
             else:
                 nc.vector.tensor_copy(out=o[:, :], in_=banks[(VCH, a)][:, :])
@@ -332,7 +332,8 @@ def tile_qwen3_5attention_pa_kernel(
         pending = []
         x_ready = []
         sq_todo = [(ci, a) for ci in range(5) for a in range(TT)]
-        norm_todo = [(ci, a) for ci in range(6) for a in range(TT)]
+        norm_todo = [(ci, a) for ci in range(5 if G_ASSIST else 6) for a in range(TT)]
+        v_todo = [a for a in range(TT) if G_ASSIST]
         sq_done = []
         mm_left = {}
         for ci in range(6):
@@ -443,4 +444,8 @@ def tile_qwen3_5attention_pa_kernel(
                     if ci != VCH:
                         norm_c(ci, a, half)
             run_matmuls()
-        assert not pending and not norm_todo and not sq_todo
+            for a in list(v_todo):
+                if mm_left[(VCH, a)] == 0 and not sq_todo and not roots:
+                    value_out(a)
+                    v_todo.remove(a)
+        assert not pending and not norm_todo and not sq_todo and not v_todo

@@ -30,11 +30,12 @@ G_ASSIST = True
 S_INTERLEAVES = [(4, 3)]
 V_AT = [14, 18, 22, 23]
 HEAD = [(0, 0), (0, 1), (1, 0), (0, 2), (1, 1), (0, 3), (1, 2), (1, 3)]
-LOADS = ["k0", "q0", "k1", "q1", "x0", "k2", "q2", "x1", "k3", "q3", "x2", "x3"]
+LOADS = ["q0", "k0", "k1", "q1", "x0", "k2", "q2", "x1", "k3", "q3", "x2", "x3"]
 X_AFTER = [2, 4, 5, 6]
+IL_RUN = 4
 WIDE_BUFS = 4
 GROUPED_BUFS = 4
-OUT_BUFS = 8
+OUT_BUFS = 4
 WV_LOAD_AFTER = 1
 LOOK = 2
 D_SQ = 3
@@ -65,6 +66,7 @@ def tile_qwen3_5attention_pa_kernel(
         wq_bytes = keep.tile([P, 4, PASSES, 4, CW], U8, name="wq_bytes")
         wq_scale = keep.tile([P, PASSES, 4], F32, name="wq_scale")
         wk_sb = keep.tile([P, PASSES, 4, CW], BF16, name="wk_sb")
+        wk_first = keep.tile([P, 2, 4, CW // 2], BF16, name="wk_first")
         wv_sb = keep.tile([P, PASSES, 4, CW], BF16, name="wv_sb")
         w_codes = keep.tile([P, 6, PASSES, CW], U32, name="w_codes", align_bytes=64)
         w_scales = keep.tile([P, 6, PASSES, CW], U8, name="w_scales", align_bytes=64)
@@ -103,7 +105,11 @@ def tile_qwen3_5attention_pa_kernel(
         make_identity(nc, ident[:])
         for what in LOADS:
             s = int(what[1])
-            if what[0] == "k":
+            if what == "k0":
+                for half in range(2):
+                    cols = slice(half * 256, half * 256 + 256)
+                    nc.sync.dma_start(out=wk_first[:, half], in_=wk_dram[s][:, :, cols])
+            elif what[0] == "k":
                 nc.sync.dma_start(out=wk_sb[:, s], in_=wk_dram[s])
             elif what[0] == "q":
                 load_wq(0, s)
@@ -152,10 +158,17 @@ def tile_qwen3_5attention_pa_kernel(
             src = wk_sb[:, g] if ci == KCH else wv_sb[:, g] if ci == VCH else wides[(ci, g)]
             if (ci, g) in S_INTERLEAVES:
                 grouped = stage.tile([P, 4 * CW], BF16, name="grouped_s", bufs=2, align_bytes=64)
-                nc.scalar.copy(out=grouped.rearrange("p (c i t) -> p c t i", i=4, t=4), in_=src.rearrange("p t (c i) -> p c t i", i=4))
+                nc.scalar.copy(out=grouped.rearrange("p (c i t) -> p c t i", i=IL_RUN, t=4), in_=src.rearrange("p t (c i) -> p c t i", i=IL_RUN))
             else:
                 grouped = stage.tile([P, 4 * CW], BF16, name="grouped", bufs=GROUPED_BUFS, align_bytes=64)
-                nc.vector.tensor_copy(out=grouped.rearrange("p (c i t) -> p c t i", i=4, t=4), in_=src.rearrange("p t (c i) -> p c t i", i=4))
+                parts = 2 if (ci, g) == (KCH, 0) else 1
+                w = CW // parts
+                for k in range(parts):
+                    part = wk_first[:, k] if parts == 2 else src
+                    nc.vector.tensor_copy(
+                        out=grouped[:, 4 * w * k : 4 * w * (k + 1)].rearrange("p (c i t) -> p c t i", i=IL_RUN, t=4),
+                        in_=part.rearrange("p t (c i) -> p c t i", i=IL_RUN),
+                    )
             groupeds[(ci, g)] = grouped
 
         def quantize(ci, g):
@@ -205,65 +218,73 @@ def tile_qwen3_5attention_pa_kernel(
                 dst = outv_dram[a]
             else:
                 dst = outq_dram[a][:, (ci - 1) * CW : ci * CW]
-            nc.sync.dma_start(out=dst, in_=o[:, :])
+            nc.sync.dma_start(out=dst, in_=o)
 
-        def squares(ci, a):
-            ss = stage.tile([P, HEADS], F32, name="ss", bufs=4)
-            for h in range(HEADS):
-                junk = stage.tile([P, HD], F32, name="junk", bufs=2)
-                nc.scalar.activation(out=junk[:], in_=banks[(ci, a)][:, h * HD : (h + 1) * HD], func=ACT.Square, accum_out=ss[:, h : h + 1])
-            stats[(ci, a)] = ss
+        def squares(group):
+            ss = stage.tile([P, RATE * HEADS], F32, name="ss", bufs=3)
+            for k in range(len(group)):
+                for h in range(HEADS):
+                    junk = stage.tile([P, HD], F32, name="junk", bufs=2)
+                    nc.scalar.activation(
+                        out=junk[:], in_=banks[group[k]][:, h * HD : (h + 1) * HD], func=ACT.Square, accum_out=ss[:, HEADS * k + h : HEADS * k + h + 1]
+                    )
+            stats[group[0]] = ss
 
-        def root(ci, a):
-            rms = stage.tile([P, HEADS], F32, name="rms", bufs=4)
-            nc.scalar.activation(out=rms[:], in_=stats[(ci, a)][:], func=ACT.Sqrt, scale=1.0 / HD, bias=EPS)
-            stats[(ci, a)] = rms
+        def root(group):
+            rms = stage.tile([P, RATE * HEADS], F32, name="rms", bufs=3)
+            m = HEADS * len(group)
+            nc.scalar.activation(out=rms[:, 0:m], in_=stats[group[0]][:, 0:m], func=ACT.Sqrt, scale=1.0 / HD, bias=EPS)
+            stats[group[0]] = rms
 
-        def norm_a(ci, a):
-            rstd = stage.tile([P, HEADS], F32, name="rstd", bufs=4)
-            nc.vector.reciprocal(out=rstd[:], in_=stats[(ci, a)][:])
-            stats[(ci, a)] = rstd
+        def norm_a(group):
+            rstd = stage.tile([P, RATE * HEADS], F32, name="rstd", bufs=3)
+            m = HEADS * len(group)
+            nc.vector.reciprocal(out=rstd[:, 0:m], in_=stats[group[0]][:, 0:m])
+            stats[group[0]] = rstd
 
-        def norm_b(ci, a):
-            qk = 1 if ci == KCH else 0
-            rstd = stats[(ci, a)]
-            o = stage.tile([P, CW], F32, name="o", bufs=OUT_BUFS)
-            ysin = stage.tile([P, HEADS, 32], F32, name="ysin", bufs=4)
-            acc = banks[(ci, a)]
-            for h in range(HEADS):
-                nc.vector.scalar_tensor_tensor(
-                    out=o[:, h * HD : (h + 1) * HD],
-                    in0=acc[:, h * HD : (h + 1) * HD],
-                    scalar=rstd[:, h : h + 1],
-                    in1=gain_cos[:, qk, a % 2, :],
-                    op0=ALU.mult,
-                    op1=ALU.mult,
-                )
-                nc.vector.scalar_tensor_tensor(
-                    out=ysin[:, h, :],
-                    in0=acc[:, h * HD : h * HD + 32],
-                    scalar=rstd[:, h : h + 1],
-                    in1=gain_sin[:, qk, a % 2, :],
-                    op0=ALU.mult,
-                    op1=ALU.mult,
-                )
-            stats[(ci, a)] = (o, ysin)
+        def norm_b(group):
+            rstd = stats[group[0]]
+            o = stage.tile([P, RATE, CW], F32, name="o", bufs=OUT_BUFS)
+            ysin = stage.tile([P, RATE * HEADS, 32], F32, name="ysin", bufs=3)
+            for k in range(len(group)):
+                ci, a = group[k]
+                qk = 1 if ci == KCH else 0
+                acc = banks[(ci, a)]
+                for h in range(HEADS):
+                    nc.vector.scalar_tensor_tensor(
+                        out=o[:, k, h * HD : (h + 1) * HD],
+                        in0=acc[:, h * HD : (h + 1) * HD],
+                        scalar=rstd[:, HEADS * k + h : HEADS * k + h + 1],
+                        in1=gain_cos[:, qk, a % 2, :],
+                        op0=ALU.mult,
+                        op1=ALU.mult,
+                    )
+                    nc.vector.scalar_tensor_tensor(
+                        out=ysin[:, HEADS * k + h, :],
+                        in0=acc[:, h * HD : h * HD + 32],
+                        scalar=rstd[:, HEADS * k + h : HEADS * k + h + 1],
+                        in1=gain_sin[:, qk, a % 2, :],
+                        op0=ALU.mult,
+                        op1=ALU.mult,
+                    )
+            stats[group[0]] = (o, ysin)
 
-        def norm_c(ci, a, half):
-            o, ysin = stats[(ci, a)]
-            oh = o.rearrange("p (h d) -> p h d", h=HEADS)
-            lo, hi = 16 * half, 16 * half + 16
-            nc.vector.tensor_tensor(out=oh[:, :, lo:hi], in0=oh[:, :, lo:hi], in1=ysin[:, :, 16 - lo : 32 - lo], op=ALU.add)
-            if half == 1:
-                store(ci, a, o)
+        def norm_c(group):
+            o, ysin = stats[group[0]]
+            m = HEADS * len(group)
+            rope = o.rearrange("p k (h d) -> p (k h) d", h=HEADS)[:, 0:m, 0:32].rearrange("p m (w i) -> p m w i", w=2)
+            swapped = ysin[:, 0:m, :].rearrange("p m (w i) -> p m w i", w=2)[:, :, ::-1, :]
+            nc.vector.tensor_tensor(out=rope, in0=rope, in1=swapped, op=ALU.add)
+            for k in range(len(group)):
+                store(group[k][0], group[k][1], o[:, k, :])
 
         def value_out(a):
-            o = stage.tile([P, CW], F32, name="o", bufs=OUT_BUFS)
+            o = stage.tile([P, CW], F32, name="o_v", bufs=4)
             if a % 2 == 0 or G_ASSIST:
                 nc.scalar.copy(out=o[:, :], in_=banks[(VCH, a)][:, :])
             else:
                 nc.vector.tensor_copy(out=o[:, :], in_=banks[(VCH, a)][:, :])
-            store(VCH, a, o)
+            store(VCH, a, o[:, :])
 
         def g_interleave(k):
             g, half = k // 2, k % 2
@@ -343,9 +364,9 @@ def tile_qwen3_5attention_pa_kernel(
         roots = []
 
         def do_roots():
-            for item in roots:
-                root(item[0], item[1])
-                sq_done.append(item)
+            for group in roots:
+                root(group)
+                sq_done.append(group)
             roots.clear()
 
         def first_stage(i):
@@ -394,11 +415,12 @@ def tile_qwen3_5attention_pa_kernel(
             return item
 
         for i in range(n + 12):
-            k = 0
-            while sq_todo and k < RATE and mm_left[sq_todo[0]] == 0 and i >= last_step[sq_todo[0][0]] + D_SQ:
-                squares(sq_todo[0][0], sq_todo[0][1])
-                roots.append(take(sq_todo))
-                k += 1
+            group = []
+            while sq_todo and len(group) < RATE and mm_left[sq_todo[0]] == 0 and i >= last_step[sq_todo[0][0]] + D_SQ:
+                group.append(take(sq_todo))
+            if group:
+                squares(group)
+                roots.append(group)
             first_stage(i + LOOK)
             if i in X_AFTER:
                 a = X_AFTER.index(i)
@@ -408,28 +430,24 @@ def tile_qwen3_5attention_pa_kernel(
                     take_x(a + 1)
                 x_copy(a)
             now = []
-            while norm_todo and len(now) < RATE and mm_left[norm_todo[0]] == 0 and i >= last_step[norm_todo[0][0]] + D_NORM:
-                if norm_todo[0][0] != VCH and norm_todo[0] not in sq_done:
-                    break
-                now.append(take(norm_todo))
-            for ci, a in now:
-                if ci != VCH:
-                    norm_a(ci, a)
+            if sq_done and i >= last_step[sq_done[0][0][0]] + D_NORM:
+                now = take(sq_done)
+                for item in now:
+                    norm_todo.remove(item)
+                norm_a(now)
             second_stage(i + 1)
             if G_ASSIST and windows[0] == 2 * PASSES:
                 g_quantize(2 * PASSES - 1)
                 windows[0] += 1
-            if G_ASSIST and now and now[0][0] != VCH:
+            if G_ASSIST and now:
                 if 0 < windows[0] < 2 * PASSES:
                     g_quantize(windows[0] - 1)
                 if windows[0] < 2 * PASSES:
                     g_interleave(windows[0])
                     windows[0] += 1
+            if now:
+                norm_b(now)
             for ci, a in now:
-                if ci == VCH:
-                    value_out(a)
-                else:
-                    norm_b(ci, a)
                 bank_user[bank_of[ci] + a] = None
                 turns_done[bank_of[ci] + a] = ci // 2 + 1
             if i < n:
@@ -439,10 +457,8 @@ def tile_qwen3_5attention_pa_kernel(
             if i - 1 in X_AFTER:
                 x_quantize(X_AFTER.index(i - 1))
                 x_ready.append(X_AFTER.index(i - 1))
-            for half in range(2):
-                for ci, a in now:
-                    if ci != VCH:
-                        norm_c(ci, a, half)
+            if now:
+                norm_c(now)
             run_matmuls()
             for a in list(v_todo):
                 if mm_left[(VCH, a)] == 0 and not sq_todo and not roots:

@@ -27,7 +27,7 @@ FLOPS = 2 * TOKENS * FEATURES * 3072
 
 KCH, VCH = 0, 5
 G_ASSIST = True
-S_INTERLEAVES = [(4, 3)]
+S_INTERLEAVES = []
 V_AT = [14, 18, 22, 23]
 HEAD = [(0, 0), (0, 1), (1, 0), (0, 2), (1, 1), (0, 3), (1, 2), (1, 3)]
 LOADS = ["q0", "k0", "k1", "q1", "x0", "k2", "q2", "x1", "k3", "q3", "x2", "x3"]
@@ -38,8 +38,8 @@ GROUPED_BUFS = 4
 OUT_BUFS = 4
 WV_LOAD_AFTER = 1
 LOOK = 2
-D_SQ = 3
-D_NORM = 4
+D_SQ = 4
+D_NORM = 5
 RATE = 2
 
 

@@ -26,21 +26,32 @@ EPS = 1e-6
 FLOPS = 2 * TOKENS * FEATURES * 3072
 
 KCH, VCH = 0, 5
-G_ASSIST = True
-S_INTERLEAVES = []
-V_AT = [14, 18, 22, 23]
+T_UNITS = []
+V_WIDENS = []
+EVAC_COLS = 1024
 HEAD = [(0, 0), (0, 1), (1, 0), (0, 2), (1, 1), (0, 3), (1, 2), (1, 3)]
 LOADS = ["q0", "k0", "k1", "q1", "x0", "k2", "q2", "x1", "k3", "q3", "x2", "x3"]
-X_AFTER = [2, 4, 5, 6]
+X_COPY = [1, 3, 4, 5]
+X_QUANT = [3, 5, 6, 7]
+X_BANKS = [(6, 7), (2, 3), (6, 7), (2, 3)]
+GAIN_BANK = 5
+GAIN_STEP = 5
 IL_RUN = 4
 WIDE_BUFS = 4
 GROUPED_BUFS = 4
 OUT_BUFS = 4
 WV_LOAD_AFTER = 1
-LOOK = 2
-D_SQ = 4
+LOOK = 3
+LOOK_MAX = 3
+D_SQ = 3
 D_NORM = 5
 RATE = 2
+
+
+def acc_bank(ci, a):
+    if ci == VCH:
+        return (6, 7, 2, 3)[a]
+    return (TT * ci + a) % 6
 
 
 def tile_qwen3_5attention_pa_kernel(
@@ -73,6 +84,7 @@ def tile_qwen3_5attention_pa_kernel(
         x_codes = keep.tile([P, TT, PASSES, P], U32, name="x_codes", align_bytes=64)
         x_scales = keep.tile([P, TT, PASSES, P], U8, name="x_scales", align_bytes=64)
         ident = keep.tile([P, P], F32, name="ident")
+        ident_bf = keep.tile([P, P], BF16, name="ident_bf")
         ones = keep.tile([P, P], BF16, name="ones")
         gain_rows = keep.tile([P, 2 * HD], BF16, name="gain_rows")
         pos_i = keep.tile([P, 4, 16], I32, name="pos_i")
@@ -103,6 +115,7 @@ def tile_qwen3_5attention_pa_kernel(
         nc.scalar.dma_start(out=gain_rows[0:1, HD : 2 * HD], in_=k_scale.unsqueeze(0))
         nc.gpsimd.memset(ones[:], 1.0)
         make_identity(nc, ident[:])
+        make_identity(nc, ident_bf[:])
         for what in LOADS:
             s = int(what[1])
             if what == "k0":
@@ -135,10 +148,14 @@ def tile_qwen3_5attention_pa_kernel(
         nc.scalar.activation(
             out=trig[:, :, 0:2, :], in_=wrapped[:].rearrange("p (j b) i -> p j b i", j=2), func=ACT.Sin, scale=-2.0 * math.pi
         )
-        nc.scalar.activation(out=warm[:], in_=one[:], func=ACT.Sqrt)
+        nc.scalar.activation(out=warm[:], in_=one[:], func=ACT.Abs_reciprocal_sqrt)
         nc.gpsimd.tensor_scalar(out=trig[:, :, 2, :], in0=trig[:, :, 0, :], scalar1=-1.0, scalar2=0.0, op0=ALU.mult, op1=ALU.add)
 
         wides = {}
+        live = []
+        made = []
+        bank_user = {}
+        staging_left = [len(T_UNITS)]
         groupeds = {}
         banks = {}
         x_groupeds = {}
@@ -154,25 +171,61 @@ def tile_qwen3_5attention_pa_kernel(
                     between()
             wides[(ci, g)] = wide
 
-        def interleave(ci, g):
-            src = wk_sb[:, g] if ci == KCH else wv_sb[:, g] if ci == VCH else wides[(ci, g)]
-            if (ci, g) in S_INTERLEAVES:
-                grouped = stage.tile([P, 4 * CW], BF16, name="grouped_s", bufs=2, align_bytes=64)
-                nc.scalar.copy(out=grouped.rearrange("p (c i t) -> p c t i", i=IL_RUN, t=4), in_=src.rearrange("p t (c i) -> p c t i", i=IL_RUN))
-            else:
-                grouped = stage.tile([P, 4 * CW], BF16, name="grouped", bufs=GROUPED_BUFS, align_bytes=64)
-                parts = 2 if (ci, g) == (KCH, 0) else 1
-                w = CW // parts
-                for k in range(parts):
-                    part = wk_first[:, k] if parts == 2 else src
-                    nc.vector.tensor_copy(
-                        out=grouped[:, 4 * w * k : 4 * w * (k + 1)].rearrange("p (c i t) -> p c t i", i=IL_RUN, t=4),
-                        in_=part.rearrange("p t (c i) -> p c t i", i=IL_RUN),
-                    )
+        def widen_v(ci, g):
+            wide = stage.tile([P, 4, CW], BF16, name="wide", bufs=WIDE_BUFS)
+            for t in range(4):
+                nc.vector.tensor_scalar(
+                    out=wide[:, t, :], in0=wq_bytes[:, ci - 1, g, t, :].bitcast(FP8), scalar1=wq_scale[:, g, t : t + 1], scalar2=None, op0=ALU.mult
+                )
+            wides[(ci, g)] = wide
+
+        def new_grouped(ci, g):
+            live.append((ci, g))
+            made.append((ci, g))
+            assert len(made) <= GROUPED_BUFS or made[len(made) - 1 - GROUPED_BUFS] not in live
+            grouped = stage.tile([P, 4 * CW], BF16, name="grouped", bufs=GROUPED_BUFS, align_bytes=64)
             groupeds[(ci, g)] = grouped
+            return grouped
+
+        def interleave(ci, g):
+            src = wk_sb[:, g] if ci == KCH else wides[(ci, g)]
+            grouped = new_grouped(ci, g)
+            parts = 2 if (ci, g) == (KCH, 0) else 1
+            w = CW // parts
+            for k in range(parts):
+                part = wk_first[:, k] if parts == 2 else src
+                nc.vector.tensor_copy(
+                    out=grouped[:, 4 * w * k : 4 * w * (k + 1)].rearrange("p (c i t) -> p c t i", i=IL_RUN, t=4),
+                    in_=part.rearrange("p t (c i) -> p c t i", i=IL_RUN),
+                )
+
+        def t_interleave(ci, g):
+            src = wk_sb[:, g] if ci == KCH else wides[(ci, g)]
+            for half in range(2):
+                assert bank_user.get(6 + half) is None
+                stg = psum.tile([P, 2 * CW], BF16, name="bank%d" % (6 + half), tag="bank%d" % (6 + half))
+                for k in range(2):
+                    c0 = 256 * half + 128 * k
+                    nc.tensor.matmul(
+                        out=stg[:, CW * k : CW * (k + 1)].rearrange("p (c t) -> p c t", t=4),
+                        lhsT=ident_bf[:],
+                        rhs=src[:, :, c0 : c0 + 128].rearrange("p t c -> p c t"),
+                        start=True,
+                        stop=True,
+                    )
+                banks[("t", half)] = stg
+                bank_user[6 + half] = ("t", ci, g)
+
+        def t_empty(ci, g):
+            grouped = new_grouped(ci, g)
+            for half in range(2):
+                nc.scalar.copy(out=grouped[:, 2 * CW * half : 2 * CW * half + EVAC_COLS], in_=banks[("t", half)][:, 0:EVAC_COLS])
+                bank_user[6 + half] = None
+            staging_left[0] -= 1
 
         def quantize(ci, g):
             nc.vector.quantize_mx(out=w_codes[:, ci, g, :].bitcast(FP8X4), scales=w_scales[:, ci, g, :], in_=groupeds[(ci, g)][:, :])
+            live.remove((ci, g))
 
         def multiply(ci, g, a):
             nc.tensor.matmul_mx(
@@ -188,7 +241,7 @@ def tile_qwen3_5attention_pa_kernel(
         def x_transpose(a):
             words = x_sb[:, a, :].bitcast(F32)
             for half in range(2):
-                xt = bank(a + 4 * half)
+                xt = bank(X_BANKS[a][half])
                 xt4 = xt.rearrange("p (c r) -> p c r", c=4)
                 for c in range(4):
                     g, u = 2 * half + c // 2, c % 2
@@ -231,15 +284,9 @@ def tile_qwen3_5attention_pa_kernel(
             stats[group[0]] = ss
 
         def root(group):
-            rms = stage.tile([P, RATE * HEADS], F32, name="rms", bufs=3)
-            m = HEADS * len(group)
-            nc.scalar.activation(out=rms[:, 0:m], in_=stats[group[0]][:, 0:m], func=ACT.Sqrt, scale=1.0 / HD, bias=EPS)
-            stats[group[0]] = rms
-
-        def norm_a(group):
             rstd = stage.tile([P, RATE * HEADS], F32, name="rstd", bufs=3)
             m = HEADS * len(group)
-            nc.vector.reciprocal(out=rstd[:, 0:m], in_=stats[group[0]][:, 0:m])
+            nc.scalar.activation(out=rstd[:, 0:m], in_=stats[group[0]][:, 0:m], func=ACT.Abs_reciprocal_sqrt, scale=1.0 / HD, bias=EPS)
             stats[group[0]] = rstd
 
         def norm_b(group):
@@ -280,10 +327,7 @@ def tile_qwen3_5attention_pa_kernel(
 
         def value_out(a):
             o = stage.tile([P, CW], F32, name="o_v", bufs=4)
-            if a % 2 == 0 or G_ASSIST:
-                nc.scalar.copy(out=o[:, :], in_=banks[(VCH, a)][:, :])
-            else:
-                nc.vector.tensor_copy(out=o[:, :], in_=banks[(VCH, a)][:, :])
+            nc.scalar.copy(out=o[:, :], in_=banks[(VCH, a)][:, :])
             store(VCH, a, o[:, :])
 
         def g_interleave(k):
@@ -310,7 +354,7 @@ def tile_qwen3_5attention_pa_kernel(
                     pending.append((VCH, g, a))
 
         def gain_matmul():
-            gb = bank(7)
+            gb = bank(GAIN_BANK)
             nc.tensor.matmul(out=gb[:, 0 : 2 * HD], lhsT=ones[:], rhs=gain_rows[:], start=True, stop=True)
             banks["gains"] = gb
 
@@ -332,29 +376,26 @@ def tile_qwen3_5attention_pa_kernel(
 
         units = list(HEAD)
         units.extend([(ci, g) for ci in range(2, 5) for g in range(PASSES)])
-        if not G_ASSIST:
-            others = list(units)
-            units.clear()
-            for i in range(len(others) + PASSES):
-                if i in V_AT:
-                    units.append((VCH, V_AT.index(i)))
-                else:
-                    units.append(others[i - len([v for v in V_AT if v < i])])
         n = len(units)
         last_step = {}
         for i in range(n):
             last_step[units[i][0]] = i
-        if G_ASSIST:
-            last_step[VCH] = 0
+        last_step[VCH] = 0
+        s_units = [u for u in units if u in T_UNITS or (u[0] != KCH and u not in V_WIDENS)]
+        s_step = {}
+        for k in range(len(s_units)):
+            at = units.index(s_units[k])
+            s_step[s_units[k]] = at - LOOK if k == 0 else max(at - LOOK_MAX, min(at - LOOK, s_step[s_units[k - 1]] + 1))
         windows = [0]
-        bank_of = {0: 0, 1: 4, 2: 0, 3: 4, 4: 0, 5: 4}
-        bank_user = {}
-        turns_done = {}
+        bank_queue = {}
+        for ci in range(6):
+            for a in range(TT):
+                bank_queue.setdefault(acc_bank(ci, a), []).append((ci, a))
         pending = []
         x_ready = []
         sq_todo = [(ci, a) for ci in range(5) for a in range(TT)]
-        norm_todo = [(ci, a) for ci in range(5 if G_ASSIST else 6) for a in range(TT)]
-        v_todo = [a for a in range(TT) if G_ASSIST]
+        norm_todo = [(ci, a) for ci in range(5) for a in range(TT)]
+        v_todo = [a for a in range(TT)]
         sq_done = []
         mm_left = {}
         for ci in range(6):
@@ -362,6 +403,7 @@ def tile_qwen3_5attention_pa_kernel(
                 mm_left[(ci, a)] = PASSES
 
         roots = []
+        to_empty = []
 
         def do_roots():
             for group in roots:
@@ -370,29 +412,38 @@ def tile_qwen3_5attention_pa_kernel(
             roots.clear()
 
         def first_stage(i):
-            if i < n:
-                ci, g = units[i]
-                if ci not in (KCH, VCH):
-                    widen(ci, g, do_roots)
-                if (ci, g) in S_INTERLEAVES:
-                    interleave(ci, g)
+            for u in s_units:
+                if s_step[u] == i:
+                    if u[0] != KCH:
+                        widen(u[0], u[1], do_roots)
+                    for e in to_empty:
+                        t_empty(e[0], e[1])
+                    to_empty.clear()
+                    if u in T_UNITS:
+                        t_interleave(u[0], u[1])
+                        to_empty.append(u)
+            for e in list(to_empty):
+                if units.index(e) - 2 <= i and s_step[e] < i:
+                    t_empty(e[0], e[1])
+                    to_empty.remove(e)
             do_roots()
 
         def second_stage(i):
-            if i < n and units[i] not in S_INTERLEAVES:
+            if i < n and units[i] not in T_UNITS:
                 interleave(units[i][0], units[i][1])
 
         def run_matmuls():
             for item in list(pending):
                 ci, g, a = item
-                b = bank_of[ci] + a
+                b = acc_bank(ci, a)
                 if a not in x_ready:
                     continue
                 if (ci, a) not in banks:
-                    if bank_user.get(b) is not None or turns_done.get(b, 0) != ci // 2:
+                    if bank_user.get(b) is not None or bank_queue[b][0] != (ci, a) or (b >= 6 and staging_left[0] > 0):
                         continue
                     banks[(ci, a)] = bank(b)
                     bank_user[b] = (ci, a)
+                    bank_queue[b].remove((ci, a))
                 if any(p[0] == ci and p[2] == a and p[1] < g for p in pending):
                     continue
                 multiply(ci, g, a)
@@ -400,19 +451,23 @@ def tile_qwen3_5attention_pa_kernel(
                 pending.remove(item)
 
         def take_x(a):
-            for half in range(2):
-                assert bank_user.get(a + 4 * half) is None
+            for b in X_BANKS[a]:
+                assert bank_user.get(b) is None
+                bank_user[b] = ("x", a)
             x_transpose(a)
 
-        gain_matmul()
-        for i in range(LOOK):
-            first_stage(i)
-        take_x(0)
-        second_stage(0)
         def take(todo):
             item = todo[0]
             todo.remove(item)
             return item
+
+        gain_matmul()
+        bank_user[GAIN_BANK] = "gains"
+        first = min(s_step[u] for u in s_units)
+        for i in range(first, 0):
+            first_stage(i)
+        take_x(0)
+        second_stage(0)
 
         for i in range(n + 12):
             group = []
@@ -421,25 +476,29 @@ def tile_qwen3_5attention_pa_kernel(
             if group:
                 squares(group)
                 roots.append(group)
-            first_stage(i + LOOK)
-            if i in X_AFTER:
-                a = X_AFTER.index(i)
+            first_stage(i)
+            if i in X_COPY:
+                a = X_COPY.index(i)
                 if a + 1 < TT:
-                    if a + 1 == 3:
-                        gain_tables()
                     take_x(a + 1)
                 x_copy(a)
+                for b in X_BANKS[a]:
+                    bank_user[b] = None
+            if i == GAIN_STEP:
+                gain_tables()
+                bank_user[GAIN_BANK] = None
             now = []
             if sq_done and i >= last_step[sq_done[0][0][0]] + D_NORM:
                 now = take(sq_done)
                 for item in now:
                     norm_todo.remove(item)
-                norm_a(now)
+            if i + 2 < n and units[i + 2] in V_WIDENS:
+                widen_v(units[i + 2][0], units[i + 2][1])
             second_stage(i + 1)
-            if G_ASSIST and windows[0] == 2 * PASSES:
+            if windows[0] == 2 * PASSES:
                 g_quantize(2 * PASSES - 1)
                 windows[0] += 1
-            if G_ASSIST and now:
+            if now:
                 if 0 < windows[0] < 2 * PASSES:
                     g_quantize(windows[0] - 1)
                 if windows[0] < 2 * PASSES:
@@ -448,15 +507,14 @@ def tile_qwen3_5attention_pa_kernel(
             if now:
                 norm_b(now)
             for ci, a in now:
-                bank_user[bank_of[ci] + a] = None
-                turns_done[bank_of[ci] + a] = ci // 2 + 1
+                bank_user[acc_bank(ci, a)] = None
             if i < n:
                 quantize(units[i][0], units[i][1])
                 for a in range(TT):
                     pending.append((units[i][0], units[i][1], a))
-            if i - 1 in X_AFTER:
-                x_quantize(X_AFTER.index(i - 1))
-                x_ready.append(X_AFTER.index(i - 1))
+            if i in X_QUANT:
+                x_quantize(X_QUANT.index(i))
+                x_ready.append(X_QUANT.index(i))
             if now:
                 norm_c(now)
             run_matmuls()
@@ -464,4 +522,4 @@ def tile_qwen3_5attention_pa_kernel(
                 if mm_left[(VCH, a)] == 0 and not sq_todo and not roots:
                     value_out(a)
                     v_todo.remove(a)
-        assert not pending and not norm_todo and not sq_todo and not v_todo
+        assert not pending and not norm_todo and not sq_todo and not v_todo and not to_empty

@@ -28,7 +28,6 @@ FLOPS = 2 * TOKENS * FEATURES * 3072
 KCH, VCH = 0, 5
 T_UNITS = []
 V_WIDENS = []
-EVAC_COLS = 1024
 HEAD = [(0, 0), (0, 1), (1, 0), (0, 2), (1, 1), (0, 3), (1, 2), (1, 3)]
 LOADS = ["q0", "k0", "k1", "q1", "x0", "k2", "q2", "x1", "k3", "q3", "x2", "x3"]
 X_COPY = [1, 3, 4, 5]
@@ -36,6 +35,7 @@ X_QUANT = [3, 5, 6, 7]
 X_BANKS = [(6, 7), (2, 3), (6, 7), (2, 3)]
 GAIN_BANK = 5
 GAIN_STEP = 5
+SIN_STEP = 0
 IL_RUN = 4
 WIDE_BUFS = 4
 GROUPED_BUFS = 4
@@ -44,8 +44,10 @@ WV_LOAD_AFTER = 1
 LOOK = 3
 LOOK_MAX = 3
 D_SQ = 3
-D_NORM = 5
+D_NORM = 4
 RATE = 2
+LATE_SUMS = False
+SPLIT_LAST = False
 
 
 def acc_bank(ci, a):
@@ -98,6 +100,7 @@ def tile_qwen3_5attention_pa_kernel(
         wrapped = keep.tile([P, 4, 16], F32, name="wrapped")
         trig = keep.tile([P, 2, 4, 16], F32, name="trig")
         warm = keep.tile([P, 1], F32, name="warm")
+        zero = keep.tile([P, 1], F32, name="zero")
         gain_cos = keep.tile([P, 2, 2, HD], F32, name="gain_cos")
         gain_sin = keep.tile([P, 2, 2, 32], F32, name="gain_sin")
 
@@ -107,12 +110,14 @@ def tile_qwen3_5attention_pa_kernel(
         def load_wq(c, g):
             nc.sync.dma_start(out=wq_bytes[:, c, g, :, :], in_=wq_dram[g][:, :, c * CW : (c + 1) * CW])
 
+        nc.gpsimd.memset(zero[:], 0.0)
         nc.scalar.dma_start(out=wq_scale[:], in_=wqs_dram)
         nc.gpsimd.memset(gain_rows[:], 0.0)
         nc.gpsimd.iota(pos_i[:].rearrange("p (j b) i -> p j b i", j=2), pattern=[[P, 2], [0, 2], [0, 16]], base=0, channel_multiplier=1)
         nc.gpsimd.iota(quarter_i[:].rearrange("p (j b) i -> p j b i", j=2), pattern=[[0, 2], [1, 2], [0, 16]], base=0, channel_multiplier=0)
         nc.scalar.dma_start(out=gain_rows[0:1, 0:HD], in_=q_scale.unsqueeze(0))
         nc.scalar.dma_start(out=gain_rows[0:1, HD : 2 * HD], in_=k_scale.unsqueeze(0))
+        nc.scalar.activation(out=warm[:], in_=zero[:], func=ACT.Sin)
         nc.gpsimd.memset(ones[:], 1.0)
         make_identity(nc, ident[:])
         make_identity(nc, ident_bf[:])
@@ -145,11 +150,12 @@ def tile_qwen3_5attention_pa_kernel(
         nc.vector.tensor_copy(out=whole_i[:], in_=turns2[:])
         nc.vector.scalar_tensor_tensor(out=frac[:], in0=whole_i[:], scalar=-1.0, in1=turns2[:], op0=ALU.mult, op1=ALU.add)
         nc.vector.scalar_tensor_tensor(out=wrapped[:], in0=frac[:], scalar=0.5, in1=frac[:], op0=ALU.is_gt, op1=ALU.subtract)
-        nc.scalar.activation(
-            out=trig[:, :, 0:2, :], in_=wrapped[:].rearrange("p (j b) i -> p j b i", j=2), func=ACT.Sin, scale=-2.0 * math.pi
-        )
-        nc.scalar.activation(out=warm[:], in_=one[:], func=ACT.Abs_reciprocal_sqrt)
-        nc.gpsimd.tensor_scalar(out=trig[:, :, 2, :], in0=trig[:, :, 0, :], scalar1=-1.0, scalar2=0.0, op0=ALU.mult, op1=ALU.add)
+
+        def sines():
+            nc.scalar.activation(
+                out=trig[:, :, 0:2, :], in_=wrapped[:].rearrange("p (j b) i -> p j b i", j=2), func=ACT.Sin, scale=-2.0 * math.pi
+            )
+            nc.gpsimd.tensor_scalar(out=trig[:, :, 2, :], in0=trig[:, :, 0, :], scalar1=-1.0, scalar2=0.0, op0=ALU.mult, op1=ALU.add)
 
         wides = {}
         live = []
@@ -219,7 +225,7 @@ def tile_qwen3_5attention_pa_kernel(
         def t_empty(ci, g):
             grouped = new_grouped(ci, g)
             for half in range(2):
-                nc.scalar.copy(out=grouped[:, 2 * CW * half : 2 * CW * half + EVAC_COLS], in_=banks[("t", half)][:, 0:EVAC_COLS])
+                nc.scalar.copy(out=grouped[:, 2 * CW * half : 2 * CW * (half + 1)].bitcast(F32), in_=banks[("t", half)][:, :].bitcast(F32))
                 bank_user[6 + half] = None
             staging_left[0] -= 1
 
@@ -321,6 +327,12 @@ def tile_qwen3_5attention_pa_kernel(
             m = HEADS * len(group)
             rope = o.rearrange("p k (h d) -> p (k h) d", h=HEADS)[:, 0:m, 0:32].rearrange("p m (w i) -> p m w i", w=2)
             swapped = ysin[:, 0:m, :].rearrange("p m (w i) -> p m w i", w=2)[:, :, ::-1, :]
+            if SPLIT_LAST and not norm_todo and not late:
+                for k in range(len(group)):
+                    part = slice(HEADS * k, HEADS * (k + 1))
+                    nc.vector.tensor_tensor(out=rope[:, part], in0=rope[:, part], in1=swapped[:, part], op=ALU.add)
+                    store(group[k][0], group[k][1], o[:, k, :])
+                return
             nc.vector.tensor_tensor(out=rope, in0=rope, in1=swapped, op=ALU.add)
             for k in range(len(group)):
                 store(group[k][0], group[k][1], o[:, k, :])
@@ -403,6 +415,7 @@ def tile_qwen3_5attention_pa_kernel(
                 mm_left[(ci, a)] = PASSES
 
         roots = []
+        late = []
         to_empty = []
 
         def do_roots():
@@ -477,6 +490,8 @@ def tile_qwen3_5attention_pa_kernel(
                 squares(group)
                 roots.append(group)
             first_stage(i)
+            if i == SIN_STEP:
+                sines()
             if i in X_COPY:
                 a = X_COPY.index(i)
                 if a + 1 < TT:
@@ -515,8 +530,14 @@ def tile_qwen3_5attention_pa_kernel(
             if i in X_QUANT:
                 x_quantize(X_QUANT.index(i))
                 x_ready.append(X_QUANT.index(i))
-            if now:
+            if now and (i < n or not LATE_SUMS):
                 norm_c(now)
+            elif now:
+                late.append(now)
+                if len(late) > 1 or not norm_todo:
+                    norm_c(take(late))
+                if late and not norm_todo:
+                    norm_c(take(late))
             run_matmuls()
             for a in list(v_todo):
                 if mm_left[(VCH, a)] == 0 and not sq_todo and not roots:

@@ -28,6 +28,8 @@ FLOPS = 2 * TOKENS * FEATURES * 3072
 KCH, VCH = 0, 5
 T_UNITS = []
 V_WIDENS = []
+V_PLANES = []
+S_IL = []
 HEAD = [(0, 0), (0, 1), (1, 0), (0, 2), (1, 1), (0, 3), (1, 2), (1, 3)]
 LOADS = ["q0", "k0", "k1", "q1", "x0", "k2", "q2", "x1", "k3", "q3", "x2", "x3"]
 X_COPY = [1, 3, 4, 5]
@@ -47,7 +49,7 @@ D_SQ = 3
 D_NORM = 4
 RATE = 2
 LATE_SUMS = False
-SPLIT_LAST = False
+SPLIT_LAST = True
 
 
 def acc_bank(ci, a):
@@ -170,9 +172,14 @@ def tile_qwen3_5attention_pa_kernel(
         def widen(ci, g, between):
             wide = stage.tile([P, 4, CW], BF16, name="wide", bufs=WIDE_BUFS)
             for t in range(4):
-                nc.scalar.activation(
-                    out=wide[:, t, :], in_=wq_bytes[:, ci - 1, g, t, :].bitcast(FP8), func=ACT.Copy, scale=wq_scale[:, g, t : t + 1]
-                )
+                if (ci, g, t) in V_PLANES:
+                    nc.vector.tensor_scalar(
+                        out=wide[:, t, :], in0=wq_bytes[:, ci - 1, g, t, :].bitcast(FP8), scalar1=wq_scale[:, g, t : t + 1], scalar2=None, op0=ALU.mult
+                    )
+                else:
+                    nc.scalar.activation(
+                        out=wide[:, t, :], in_=wq_bytes[:, ci - 1, g, t, :].bitcast(FP8), func=ACT.Copy, scale=wq_scale[:, g, t : t + 1]
+                    )
                 if t == 0:
                     between()
             wides[(ci, g)] = wide
@@ -204,6 +211,10 @@ def tile_qwen3_5attention_pa_kernel(
                     out=grouped[:, 4 * w * k : 4 * w * (k + 1)].rearrange("p (c i t) -> p c t i", i=IL_RUN, t=4),
                     in_=part.rearrange("p t (c i) -> p c t i", i=IL_RUN),
                 )
+
+        def s_interleave(ci, g):
+            grouped = new_grouped(ci, g)
+            nc.scalar.copy(out=grouped.rearrange("p (c i t) -> p c t i", i=IL_RUN, t=4), in_=wides[(ci, g)].rearrange("p t (c i) -> p c t i", i=IL_RUN))
 
         def t_interleave(ci, g):
             src = wk_sb[:, g] if ci == KCH else wides[(ci, g)]
@@ -327,7 +338,7 @@ def tile_qwen3_5attention_pa_kernel(
             m = HEADS * len(group)
             rope = o.rearrange("p k (h d) -> p (k h) d", h=HEADS)[:, 0:m, 0:32].rearrange("p m (w i) -> p m w i", w=2)
             swapped = ysin[:, 0:m, :].rearrange("p m (w i) -> p m w i", w=2)[:, :, ::-1, :]
-            if SPLIT_LAST and not norm_todo and not late:
+            if SPLIT_LAST and tail[0]:
                 for k in range(len(group)):
                     part = slice(HEADS * k, HEADS * (k + 1))
                     nc.vector.tensor_tensor(out=rope[:, part], in0=rope[:, part], in1=swapped[:, part], op=ALU.add)
@@ -416,6 +427,7 @@ def tile_qwen3_5attention_pa_kernel(
 
         roots = []
         late = []
+        tail = [False]
         to_empty = []
 
         def do_roots():
@@ -429,6 +441,8 @@ def tile_qwen3_5attention_pa_kernel(
                 if s_step[u] == i:
                     if u[0] != KCH:
                         widen(u[0], u[1], do_roots)
+                    if u in S_IL:
+                        s_interleave(u[0], u[1])
                     for e in to_empty:
                         t_empty(e[0], e[1])
                     to_empty.clear()
@@ -442,7 +456,7 @@ def tile_qwen3_5attention_pa_kernel(
             do_roots()
 
         def second_stage(i):
-            if i < n and units[i] not in T_UNITS:
+            if i < n and units[i] not in T_UNITS and units[i] not in S_IL:
                 interleave(units[i][0], units[i][1])
 
         def run_matmuls():
@@ -530,6 +544,7 @@ def tile_qwen3_5attention_pa_kernel(
             if i in X_QUANT:
                 x_quantize(X_QUANT.index(i))
                 x_ready.append(X_QUANT.index(i))
+            tail[0] = i >= n
             if now and (i < n or not LATE_SUMS):
                 norm_c(now)
             elif now:

@@ -28,7 +28,7 @@ FLOPS = 2 * TOKENS * FEATURES * 3072
 KCH, VCH = 0, 5
 T_UNITS = []
 V_WIDENS = []
-V_PLANES = []
+V_PLANES = [(1, 0, 2), (1, 0, 3)]
 S_IL = []
 HEAD = [(0, 0), (0, 1), (1, 0), (0, 2), (1, 1), (0, 3), (1, 2), (1, 3)]
 LOADS = ["q0", "k0", "k1", "q1", "x0", "k2", "q2", "x1", "k3", "q3", "x2", "x3"]
@@ -157,6 +157,7 @@ def tile_qwen3_5attention_pa_kernel(
             nc.scalar.activation(
                 out=trig[:, :, 0:2, :], in_=wrapped[:].rearrange("p (j b) i -> p j b i", j=2), func=ACT.Sin, scale=-2.0 * math.pi
             )
+            nc.scalar.activation(out=warm[:], in_=one[:], func=ACT.Abs_reciprocal_sqrt)
             nc.gpsimd.tensor_scalar(out=trig[:, :, 2, :], in0=trig[:, :, 0, :], scalar1=-1.0, scalar2=0.0, op0=ALU.mult, op1=ALU.add)
 
         wides = {}

@@ -26,8 +26,8 @@ EPS = 1e-6
 FLOPS = 2 * TOKENS * FEATURES * 3072
 
 KCH, VCH = 0, 5
-T_UNITS = []
-V_WIDENS = []
+T_UNITS = [(2, 0), (2, 2), (3, 0), (3, 2), (4, 0)]
+V_WIDENS = [(2, 1), (2, 3), (3, 1), (3, 3)]
 V_PLANES = [(1, 0, 2), (1, 0, 3)]
 S_IL = []
 HEAD = [(0, 0), (0, 1), (1, 0), (0, 2), (1, 1), (0, 3), (1, 2), (1, 3)]
@@ -45,8 +45,8 @@ OUT_BUFS = 4
 WV_LOAD_AFTER = 1
 LOOK = 3
 LOOK_MAX = 3
-D_SQ = 3
-D_NORM = 4
+D_SQ = 4
+D_NORM = 5
 RATE = 2
 LATE_SUMS = False
 SPLIT_LAST = True
@@ -225,9 +225,9 @@ def tile_qwen3_5attention_pa_kernel(
                 for k in range(2):
                     c0 = 256 * half + 128 * k
                     nc.tensor.matmul(
-                        out=stg[:, CW * k : CW * (k + 1)].rearrange("p (c t) -> p c t", t=4),
+                        out=stg[:, CW * k : CW * (k + 1)].rearrange("p (c t) -> p t c", t=4),
                         lhsT=ident_bf[:],
-                        rhs=src[:, :, c0 : c0 + 128].rearrange("p t c -> p c t"),
+                        rhs=src[:, :, c0 : c0 + 128],
                         start=True,
                         stop=True,
                     )
@@ -438,20 +438,21 @@ def tile_qwen3_5attention_pa_kernel(
             roots.clear()
 
         def first_stage(i):
+            for e in list(to_empty):
+                if units.index(e) - 1 <= i and s_step[e] < i:
+                    t_empty(e[0], e[1])
+                    to_empty.remove(e)
             for u in s_units:
                 if s_step[u] == i:
                     if u[0] != KCH:
                         widen(u[0], u[1], do_roots)
                     if u in S_IL:
                         s_interleave(u[0], u[1])
-                    for e in to_empty:
-                        t_empty(e[0], e[1])
-                    to_empty.clear()
                     if u in T_UNITS:
                         t_interleave(u[0], u[1])
                         to_empty.append(u)
             for e in list(to_empty):
-                if units.index(e) - 2 <= i and s_step[e] < i:
+                if units.index(e) - 1 <= i and s_step[e] < i:
                     t_empty(e[0], e[1])
                     to_empty.remove(e)
             do_roots()

@@ -438,16 +438,15 @@ def tile_qwen3_5attention_pa_kernel(
             roots.clear()
 
         def first_stage(i):
-            for e in list(to_empty):
-                if units.index(e) - 1 <= i and s_step[e] < i:
-                    t_empty(e[0], e[1])
-                    to_empty.remove(e)
             for u in s_units:
                 if s_step[u] == i:
                     if u[0] != KCH:
                         widen(u[0], u[1], do_roots)
                     if u in S_IL:
                         s_interleave(u[0], u[1])
+                    for e in to_empty:
+                        t_empty(e[0], e[1])
+                    to_empty.clear()
                     if u in T_UNITS:
                         t_interleave(u[0], u[1])
                         to_empty.append(u)

@@ -26,7 +26,7 @@ EPS = 1e-6
 FLOPS = 2 * TOKENS * FEATURES * 3072
 
 KCH, VCH = 0, 5
-T_UNITS = [(2, 0), (2, 2), (3, 0), (3, 2), (4, 0)]
+T_UNITS = [(2, 0), (2, 2), (3, 0), (3, 2), (4, 0), (4, 2)]
 V_WIDENS = [(2, 1), (2, 3), (3, 1), (3, 3)]
 V_PLANES = [(1, 0, 2), (1, 0, 3)]
 S_IL = []
@@ -45,8 +45,8 @@ OUT_BUFS = 4
 WV_LOAD_AFTER = 1
 LOOK = 3
 LOOK_MAX = 3
-D_SQ = 4
-D_NORM = 5
+D_SQ = [4, 4, 4, 4, 4]
+D_NORM = [5, 5, 5, 5, 5]
 RATE = 2
 LATE_SUMS = False
 SPLIT_LAST = True
@@ -54,7 +54,9 @@ SPLIT_LAST = True
 
 def acc_bank(ci, a):
     if ci == VCH:
-        return (6, 7, 2, 3)[a]
+        return a
+    if ci == 4 and a >= 2:
+        return 4 + a
     return (TT * ci + a) % 6
 
 
@@ -499,7 +501,7 @@ def tile_qwen3_5attention_pa_kernel(
 
         for i in range(n + 12):
             group = []
-            while sq_todo and len(group) < RATE and mm_left[sq_todo[0]] == 0 and i >= last_step[sq_todo[0][0]] + D_SQ:
+            while sq_todo and len(group) < RATE and mm_left[sq_todo[0]] == 0 and i >= last_step[sq_todo[0][0]] + D_SQ[sq_todo[0][0]]:
                 group.append(take(sq_todo))
             if group:
                 squares(group)
@@ -518,7 +520,7 @@ def tile_qwen3_5attention_pa_kernel(
                 gain_tables()
                 bank_user[GAIN_BANK] = None
             now = []
-            if sq_done and i >= last_step[sq_done[0][0][0]] + D_NORM:
+            if sq_done and i >= last_step[sq_done[0][0][0]] + D_NORM[sq_done[0][0][0]]:
                 now = take(sq_done)
                 for item in now:
                     norm_todo.remove(item)

@@ -28,7 +28,7 @@ FLOPS = 2 * TOKENS * FEATURES * 3072
 KCH, VCH = 0, 5
 T_UNITS = [(2, 0), (2, 2), (3, 0), (3, 2), (4, 0), (4, 2)]
 V_WIDENS = [(2, 1), (2, 3), (3, 1), (3, 3)]
-V_PLANES = [(1, 0, 2), (1, 0, 3)]
+V_PLANES = [(1, 0, 2), (1, 0, 3), (4, 1, 2), (4, 1, 3)]
 S_IL = []
 HEAD = [(0, 0), (0, 1), (1, 0), (0, 2), (1, 1), (0, 3), (1, 2), (1, 3)]
 LOADS = ["q0", "k0", "k1", "q1", "x0", "k2", "q2", "x1", "k3", "q3", "x2", "x3"]
@@ -432,6 +432,7 @@ def tile_qwen3_5attention_pa_kernel(
         late = []
         tail = [False]
         to_empty = []
+        to_il = []
 
         def do_roots():
             for group in roots:
@@ -446,16 +447,17 @@ def tile_qwen3_5attention_pa_kernel(
                         widen(u[0], u[1], do_roots)
                     if u in S_IL:
                         s_interleave(u[0], u[1])
-                    for e in to_empty:
-                        t_empty(e[0], e[1])
-                    to_empty.clear()
                     if u in T_UNITS:
-                        t_interleave(u[0], u[1])
-                        to_empty.append(u)
+                        to_il.append(u)
             for e in list(to_empty):
-                if units.index(e) - 1 <= i and s_step[e] < i:
+                if units.index(e) - 1 <= i:
                     t_empty(e[0], e[1])
                     to_empty.remove(e)
+            for u in list(to_il):
+                if not to_empty:
+                    t_interleave(u[0], u[1])
+                    to_empty.append(u)
+                    to_il.remove(u)
             do_roots()
 
         def second_stage(i):

@@ -28,7 +28,7 @@ FLOPS = 2 * TOKENS * FEATURES * 3072
 KCH, VCH = 0, 5
 T_UNITS = [(2, 0), (2, 2), (3, 0), (3, 2), (4, 0), (4, 2)]
 V_WIDENS = [(2, 1), (2, 3), (3, 1), (3, 3)]
-V_PLANES = [(1, 0, 2), (1, 0, 3), (4, 1, 2), (4, 1, 3)]
+V_PLANES = [(1, 0, 2), (1, 0, 3)]
 S_IL = []
 HEAD = [(0, 0), (0, 1), (1, 0), (0, 2), (1, 1), (0, 3), (1, 2), (1, 3)]
 LOADS = ["q0", "k0", "k1", "q1", "x0", "k2", "q2", "x1", "k3", "q3", "x2", "x3"]

@@ -83,7 +83,6 @@ def tile_qwen3_5attention_pa_kernel(
         wq_bytes = keep.tile([P, 4, PASSES, 4, CW], U8, name="wq_bytes")
         wq_scale = keep.tile([P, PASSES, 4], F32, name="wq_scale")
         wk_sb = keep.tile([P, PASSES, 4, CW], BF16, name="wk_sb")
-        wk_first = keep.tile([P, 2, 4, CW // 2], BF16, name="wk_first")
         wv_sb = keep.tile([P, PASSES, 4, CW], BF16, name="wv_sb")
         w_codes = keep.tile([P, 6, PASSES, CW], U32, name="w_codes", align_bytes=64)
         w_scales = keep.tile([P, 6, PASSES, CW], U8, name="w_scales", align_bytes=64)
@@ -127,11 +126,7 @@ def tile_qwen3_5attention_pa_kernel(
         make_identity(nc, ident_bf[:])
         for what in LOADS:
             s = int(what[1])
-            if what == "k0":
-                for half in range(2):
-                    cols = slice(half * 256, half * 256 + 256)
-                    nc.sync.dma_start(out=wk_first[:, half], in_=wk_dram[s][:, :, cols])
-            elif what[0] == "k":
+            if what[0] == "k":
                 nc.sync.dma_start(out=wk_sb[:, s], in_=wk_dram[s])
             elif what[0] == "q":
                 load_wq(0, s)
@@ -206,10 +201,10 @@ def tile_qwen3_5attention_pa_kernel(
         def interleave(ci, g):
             src = wk_sb[:, g] if ci == KCH else wides[(ci, g)]
             grouped = new_grouped(ci, g)
-            parts = 2 if (ci, g) == (KCH, 0) else 1
+            parts = 1
             w = CW // parts
             for k in range(parts):
-                part = wk_first[:, k] if parts == 2 else src
+                part = src
                 nc.vector.tensor_copy(
                     out=grouped[:, 4 * w * k : 4 * w * (k + 1)].rearrange("p (c i t) -> p c t i", i=IL_RUN, t=4),
                     in_=part.rearrange("p t (c i) -> p c t i", i=IL_RUN),

from contextlib import ExitStack
import math

import concourse.mybir as mybir
from concourse.masks import make_identity

F32 = mybir.dt.float32
BF16 = mybir.dt.bfloat16
I32 = mybir.dt.int32
U32 = mybir.dt.uint32
U8 = mybir.dt.uint8
FP8 = mybir.dt.float8_e4m3fn
FP8X4 = mybir.dt.float8_e4m3fn_x4
ACT = mybir.ActivationFunctionType
ALU = mybir.AluOpType

P = 128
TOKENS = 512
FEATURES = 2048
PASSES = 4
TT = 4
CW = 512
HD = 128
HEADS = 4
EPS = 1e-6
FLOPS = 2 * TOKENS * FEATURES * 3072

KCH, VCH = 0, 5
T_UNITS = [(2, 0), (2, 2), (3, 0), (3, 2), (4, 0), (4, 2)]
V_WIDENS = [(2, 1), (2, 3), (3, 1), (3, 3)]
V_PLANES = [(1, 0, 2), (1, 0, 3)]
S_IL = []
HEAD = [(0, 0), (0, 1), (1, 0), (0, 2), (1, 1), (0, 3), (1, 2), (1, 3)]
LOADS = ["q0", "k0", "k1", "q1", "x0", "k2", "q2", "x1", "k3", "q3", "x2", "x3"]
X_COPY = [1, 3, 4, 5]
X_QUANT = [3, 5, 6, 7]
X_BANKS = [(6, 7), (2, 3), (6, 7), (2, 3)]
GAIN_BANK = 5
GAIN_STEP = 5
SIN_STEP = 0
IL_RUN = 4
WIDE_BUFS = 4
GROUPED_BUFS = 4
OUT_BUFS = 4
WV_LOAD_AFTER = 1
LOOK = 3
LOOK_MAX = 3
D_SQ = [4, 4, 4, 4, 4]
D_NORM = [5, 5, 5, 5, 5]
RATE = 2
LATE_SUMS = False
SPLIT_LAST = True


def acc_bank(ci, a):
    if ci == VCH:
        return a
    if ci == 4 and a >= 2:
        return 4 + a
    return (TT * ci + a) % 6


def tile_qwen3_5attention_pa_kernel(
    tc, hidden_states, Wq_query_bytes, Wq_query_scale, Wk, Wv, q_scale, k_scale, out_0, out_1, out_2
):
    nc = tc.nc
    x_dram = hidden_states.flatten_outer_dims().rearrange("(a p) k -> a p k", p=P)
    wq_dram = Wq_query_bytes.rearrange("(g p t) u h -> g p t (u h)", p=P, t=4)
    wqs_dram = Wq_query_scale.rearrange("(g p t) a b -> p g (t a b)", p=P, t=4)
    wk_dram = Wk.rearrange("(g p t) u h -> g p t (u h)", p=P, t=4)
    wv_dram = Wv.rearrange("(g p t) u h -> g p t (u h)", p=P, t=4)
    outq_dram = out_0.rearrange("b s u h -> (b s) (u h)").rearrange("(a p) c -> a p c", p=P)
    outk_dram = out_1.rearrange("b s u h -> (b s) (u h)").rearrange("(a p) c -> a p c", p=P)
    outv_dram = out_2.rearrange("b s u h -> (b s) (u h)").rearrange("(a p) c -> a p c", p=P)

    with ExitStack() as ctx:
        keep = ctx.enter_context(tc.tile_pool(name="keep", bufs=1))
        stage = ctx.enter_context(tc.tile_pool(name="stage", bufs=2))
        psum = ctx.enter_context(tc.psum_pool(name="psum", bufs=1))
        ctx.enter_context(tc.manual_schedule())

        x_sb = keep.tile([P, TT, FEATURES], BF16, name="x_sb")
        wq_bytes = keep.tile([P, 4, PASSES, 4, CW], U8, name="wq_bytes")
        wq_scale = keep.tile([P, PASSES, 4], F32, name="wq_scale")
        wk_sb = keep.tile([P, PASSES, 4, CW], BF16, name="wk_sb")
        wv_sb = keep.tile([P, PASSES, 4, CW], BF16, name="wv_sb")
        w_codes = keep.tile([P, 6, PASSES, CW], U32, name="w_codes", align_bytes=64)
        w_scales = keep.tile([P, 6, PASSES, CW], U8, name="w_scales", align_bytes=64)
        x_codes = keep.tile([P, TT, PASSES, P], U32, name="x_codes", align_bytes=64)
        x_scales = keep.tile([P, TT, PASSES, P], U8, name="x_scales", align_bytes=64)
        ident = keep.tile([P, P], F32, name="ident")
        ident_bf = keep.tile([P, P], BF16, name="ident_bf")
        ones = keep.tile([P, P], BF16, name="ones")
        gain_rows = keep.tile([P, 2 * HD], BF16, name="gain_rows")
        pos_i = keep.tile([P, 4, 16], I32, name="pos_i")
        quarter_i = keep.tile([P, 4, 16], I32, name="quarter_i")
        tau = keep.tile([P, 16], F32, name="tau")
        one = keep.tile([P, 1], F32, name="one")
        turns = keep.tile([P, 4, 16], F32, name="turns")
        turns2 = keep.tile([P, 4, 16], F32, name="turns2")
        whole_i = keep.tile([P, 4, 16], I32, name="whole_i")
        frac = keep.tile([P, 4, 16], F32, name="frac")
        wrapped = keep.tile([P, 4, 16], F32, name="wrapped")
        trig = keep.tile([P, 2, 4, 16], F32, name="trig")
        warm = keep.tile([P, 1], F32, name="warm")
        zero = keep.tile([P, 1], F32, name="zero")
        gain_cos = keep.tile([P, 2, 2, HD], F32, name="gain_cos")
        gain_sin = keep.tile([P, 2, 2, 32], F32, name="gain_sin")

        def bank(b):
            return psum.tile([P, CW], F32, name="bank%d" % b, tag="bank%d" % b)

        def load_wq(c, g):
            nc.sync.dma_start(out=wq_bytes[:, c, g, :, :], in_=wq_dram[g][:, :, c * CW : (c + 1) * CW])

        nc.gpsimd.memset(zero[:], 0.0)
        nc.scalar.dma_start(out=wq_scale[:], in_=wqs_dram)
        nc.gpsimd.memset(gain_rows[:], 0.0)
        nc.gpsimd.iota(pos_i[:].rearrange("p (j b) i -> p j b i", j=2), pattern=[[P, 2], [0, 2], [0, 16]], base=0, channel_multiplier=1)
        nc.gpsimd.iota(quarter_i[:].rearrange("p (j b) i -> p j b i", j=2), pattern=[[0, 2], [1, 2], [0, 16]], base=0, channel_multiplier=0)
        nc.scalar.dma_start(out=gain_rows[0:1, 0:HD], in_=q_scale.unsqueeze(0))
        nc.scalar.dma_start(out=gain_rows[0:1, HD : 2 * HD], in_=k_scale.unsqueeze(0))
        nc.scalar.activation(out=warm[:], in_=zero[:], func=ACT.Sin)
        nc.gpsimd.memset(ones[:], 1.0)
        make_identity(nc, ident[:])
        make_identity(nc, ident_bf[:])
        for what in LOADS:
            s = int(what[1])
            if what[0] == "k":
                nc.sync.dma_start(out=wk_sb[:, s], in_=wk_dram[s])
            elif what[0] == "q":
                load_wq(0, s)
            else:
                nc.sync.dma_start(out=x_sb[:, s, :], in_=x_dram[s])
        for c in range(1, 4):
            for g in range(PASSES):
                load_wq(c, g)
            if c == WV_LOAD_AFTER:
                for g in range(PASSES):
                    nc.sync.dma_start(out=wv_sb[:, g], in_=wv_dram[g])

        ratio = 10000.0 ** (-1.0 / 16.0)
        nc.vector.memset(one[:], 1.0)
        nc.vector.tensor_scalar(out=tau[:, 0:1], in0=one[:], scalar1=1.0 / (2.0 * math.pi), scalar2=None, op0=ALU.mult)
        for w in (1, 2, 4, 8):
            nc.vector.tensor_scalar(out=tau[:, w : 2 * w], in0=tau[:, 0:w], scalar1=ratio**w, scalar2=None, op0=ALU.mult)
        nc.vector.tensor_tensor(out=turns[:], in0=pos_i[:], in1=tau[:].unsqueeze(1).to_broadcast([P, 4, 16]), op=ALU.mult)
        nc.vector.scalar_tensor_tensor(out=turns2[:], in0=quarter_i[:], scalar=0.25, in1=turns[:], op0=ALU.mult, op1=ALU.add)
        nc.vector.tensor_copy(out=whole_i[:], in_=turns2[:])
        nc.vector.scalar_tensor_tensor(out=frac[:], in0=whole_i[:], scalar=-1.0, in1=turns2[:], op0=ALU.mult, op1=ALU.add)
        nc.vector.scalar_tensor_tensor(out=wrapped[:], in0=frac[:], scalar=0.5, in1=frac[:], op0=ALU.is_gt, op1=ALU.subtract)

        def sines():
            nc.scalar.activation(
                out=trig[:, :, 0:2, :], in_=wrapped[:].rearrange("p (j b) i -> p j b i", j=2), func=ACT.Sin, scale=-2.0 * math.pi
            )
            nc.scalar.activation(out=warm[:], in_=one[:], func=ACT.Abs_reciprocal_sqrt)
            nc.gpsimd.tensor_scalar(out=trig[:, :, 2, :], in0=trig[:, :, 0, :], scalar1=-1.0, scalar2=0.0, op0=ALU.mult, op1=ALU.add)

        wides = {}
        live = []
        made = []
        bank_user = {}
        staging_left = [len(T_UNITS)]
        groupeds = {}
        banks = {}
        x_groupeds = {}
        stats = {}

        def widen(ci, g, between):
            wide = stage.tile([P, 4, CW], BF16, name="wide", bufs=WIDE_BUFS)
            for t in range(4):
                if (ci, g, t) in V_PLANES:
                    nc.vector.tensor_scalar(
                        out=wide[:, t, :], in0=wq_bytes[:, ci - 1, g, t, :].bitcast(FP8), scalar1=wq_scale[:, g, t : t + 1], scalar2=None, op0=ALU.mult
                    )
                else:
                    nc.scalar.activation(
                        out=wide[:, t, :], in_=wq_bytes[:, ci - 1, g, t, :].bitcast(FP8), func=ACT.Copy, scale=wq_scale[:, g, t : t + 1]
                    )
                if t == 0:
                    between()
            wides[(ci, g)] = wide

        def widen_v(ci, g):
            wide = stage.tile([P, 4, CW], BF16, name="wide", bufs=WIDE_BUFS)
            for t in range(4):
                nc.vector.tensor_scalar(
                    out=wide[:, t, :], in0=wq_bytes[:, ci - 1, g, t, :].bitcast(FP8), scalar1=wq_scale[:, g, t : t + 1], scalar2=None, op0=ALU.mult
                )
            wides[(ci, g)] = wide

        def new_grouped(ci, g):
            live.append((ci, g))
            made.append((ci, g))
            assert len(made) <= GROUPED_BUFS or made[len(made) - 1 - GROUPED_BUFS] not in live
            grouped = stage.tile([P, 4 * CW], BF16, name="grouped", bufs=GROUPED_BUFS, align_bytes=64)
            groupeds[(ci, g)] = grouped
            return grouped

        def interleave(ci, g):
            src = wk_sb[:, g] if ci == KCH else wides[(ci, g)]
            grouped = new_grouped(ci, g)
            parts = 1
            w = CW // parts
            for k in range(parts):
                part = src
                nc.vector.tensor_copy(
                    out=grouped[:, 4 * w * k : 4 * w * (k + 1)].rearrange("p (c i t) -> p c t i", i=IL_RUN, t=4),
                    in_=part.rearrange("p t (c i) -> p c t i", i=IL_RUN),
                )

        def s_interleave(ci, g):
            grouped = new_grouped(ci, g)
            nc.scalar.copy(out=grouped.rearrange("p (c i t) -> p c t i", i=IL_RUN, t=4), in_=wides[(ci, g)].rearrange("p t (c i) -> p c t i", i=IL_RUN))

        def t_interleave(ci, g):
            src = wk_sb[:, g] if ci == KCH else wides[(ci, g)]
            for half in range(2):
                assert bank_user.get(6 + half) is None
                stg = psum.tile([P, 2 * CW], BF16, name="bank%d" % (6 + half), tag="bank%d" % (6 + half))
                for k in range(2):
                    c0 = 256 * half + 128 * k
                    nc.tensor.matmul(
                        out=stg[:, CW * k : CW * (k + 1)].rearrange("p (c t) -> p t c", t=4),
                        lhsT=ident_bf[:],
                        rhs=src[:, :, c0 : c0 + 128],
                        start=True,
                        stop=True,
                    )
                banks[("t", half)] = stg
                bank_user[6 + half] = ("t", ci, g)

        def t_empty(ci, g):
            grouped = new_grouped(ci, g)
            for half in range(2):
                nc.scalar.copy(out=grouped[:, 2 * CW * half : 2 * CW * (half + 1)].bitcast(F32), in_=banks[("t", half)][:, :].bitcast(F32))
                bank_user[6 + half] = None
            staging_left[0] -= 1

        def quantize(ci, g):
            nc.vector.quantize_mx(out=w_codes[:, ci, g, :].bitcast(FP8X4), scales=w_scales[:, ci, g, :], in_=groupeds[(ci, g)][:, :])
            live.remove((ci, g))

        def multiply(ci, g, a):
            nc.tensor.matmul_mx(
                out=banks[(ci, a)][:, :],
                lhsT=x_codes[:, a, g, :].bitcast(FP8X4),
                lhsT_scale=x_scales[:, a, g, :],
                rhs=w_codes[:, ci, g, :].bitcast(FP8X4),
                rhs_scale=w_scales[:, ci, g, :],
                start=(g == 0),
                stop=(g == PASSES - 1),
            )

        def x_transpose(a):
            words = x_sb[:, a, :].bitcast(F32)
            for half in range(2):
                xt = bank(X_BANKS[a][half])
                xt4 = xt.rearrange("p (c r) -> p c r", c=4)
                for c in range(4):
                    g, u = 2 * half + c // 2, c % 2
                    nc.tensor.transpose(xt4[:, c, :], words[:, 256 * g + u : 256 * (g + 1) : 2], ident[:])
                banks[("x", a, half)] = xt

        def x_copy(a):
            xg = stage.tile([P, PASSES, P, 4], BF16, name="x_grouped", bufs=2, align_bytes=64)
            x_groupeds[a] = xg
            for half in range(2):
                nc.scalar.copy(
                    out=xg[:, 2 * half : 2 * half + 2].rearrange("p g r t -> p g (r t)").bitcast(F32).rearrange("p g (r u) -> p g r u", u=2),
                    in_=banks[("x", a, half)].rearrange("p (g u r) -> p g r u", g=2, u=2),
                )

        def x_quantize(a):
            nc.vector.quantize_mx(
                out=x_codes[:, a].rearrange("p g r -> p (g r)").bitcast(FP8X4),
                scales=x_scales[:, a].rearrange("p g r -> p (g r)"),
                in_=x_groupeds[a].rearrange("p g r t -> p (g r t)"),
            )

        def store(ci, a, o):
            if ci == KCH:
                dst = outk_dram[a]
            elif ci == VCH:
                dst = outv_dram[a]
            else:
                dst = outq_dram[a][:, (ci - 1) * CW : ci * CW]
            nc.sync.dma_start(out=dst, in_=o)

        def squares(group):
            ss = stage.tile([P, RATE * HEADS], F32, name="ss", bufs=3)
            for k in range(len(group)):
                for h in range(HEADS):
                    junk = stage.tile([P, HD], F32, name="junk", bufs=2)
                    nc.scalar.activation(
                        out=junk[:], in_=banks[group[k]][:, h * HD : (h + 1) * HD], func=ACT.Square, accum_out=ss[:, HEADS * k + h : HEADS * k + h + 1]
                    )
            stats[group[0]] = ss

        def root(group):
            rstd = stage.tile([P, RATE * HEADS], F32, name="rstd", bufs=3)
            m = HEADS * len(group)
            nc.scalar.activation(out=rstd[:, 0:m], in_=stats[group[0]][:, 0:m], func=ACT.Abs_reciprocal_sqrt, scale=1.0 / HD, bias=EPS)
            stats[group[0]] = rstd

        def norm_b(group):
            rstd = stats[group[0]]
            o = stage.tile([P, RATE, CW], F32, name="o", bufs=OUT_BUFS)
            ysin = stage.tile([P, RATE * HEADS, 32], F32, name="ysin", bufs=3)
            for k in range(len(group)):
                ci, a = group[k]
                qk = 1 if ci == KCH else 0
                acc = banks[(ci, a)]
                for h in range(HEADS):
                    nc.vector.scalar_tensor_tensor(
                        out=o[:, k, h * HD : (h + 1) * HD],
                        in0=acc[:, h * HD : (h + 1) * HD],
                        scalar=rstd[:, HEADS * k + h : HEADS * k + h + 1],
                        in1=gain_cos[:, qk, a % 2, :],
                        op0=ALU.mult,
                        op1=ALU.mult,
                    )
                    nc.vector.scalar_tensor_tensor(
                        out=ysin[:, HEADS * k + h, :],
                        in0=acc[:, h * HD : h * HD + 32],
                        scalar=rstd[:, HEADS * k + h : HEADS * k + h + 1],
                        in1=gain_sin[:, qk, a % 2, :],
                        op0=ALU.mult,
                        op1=ALU.mult,
                    )
            stats[group[0]] = (o, ysin)

        def norm_c(group):
            o, ysin = stats[group[0]]
            m = HEADS * len(group)
            rope = o.rearrange("p k (h d) -> p (k h) d", h=HEADS)[:, 0:m, 0:32].rearrange("p m (w i) -> p m w i", w=2)
            swapped = ysin[:, 0:m, :].rearrange("p m (w i) -> p m w i", w=2)[:, :, ::-1, :]
            if SPLIT_LAST and tail[0]:
                for k in range(len(group)):
                    part = slice(HEADS * k, HEADS * (k + 1))
                    nc.vector.tensor_tensor(out=rope[:, part], in0=rope[:, part], in1=swapped[:, part], op=ALU.add)
                    store(group[k][0], group[k][1], o[:, k, :])
                return
            nc.vector.tensor_tensor(out=rope, in0=rope, in1=swapped, op=ALU.add)
            for k in range(len(group)):
                store(group[k][0], group[k][1], o[:, k, :])

        def value_out(a):
            o = stage.tile([P, CW], F32, name="o_v", bufs=4)
            nc.scalar.copy(out=o[:, :], in_=banks[(VCH, a)][:, :])
            store(VCH, a, o[:, :])

        def g_interleave(k):
            g, half = k // 2, k % 2
            grouped = stage.tile([P, 2 * CW], BF16, name="grouped_g", bufs=1, align_bytes=64)
            if k == 0:
                nc.vector.memset(grouped[:, 0:2], 1.0)
            nc.gpsimd.tensor_scalar(
                out=grouped.rearrange("p (n t) -> p n t", t=4),
                in0=wv_sb[:, g, :, half * 256 : half * 256 + 256].rearrange("p t n -> p n t"),
                scalar1=1.0,
                scalar2=0.0,
                op0=ALU.mult,
                op1=ALU.add,
            )
            groupeds[("g", k)] = grouped

        def g_quantize(k):
            g, half = k // 2, k % 2
            cols = slice(half * 256, half * 256 + 256)
            nc.vector.quantize_mx(out=w_codes[:, VCH, g, cols].bitcast(FP8X4), scales=w_scales[:, VCH, g, cols], in_=groupeds[("g", k)][:, :])
            if half == 1:
                for a in range(TT):
                    pending.append((VCH, g, a))

        def gain_matmul():
            gb = bank(GAIN_BANK)
            nc.tensor.matmul(out=gb[:, 0 : 2 * HD], lhsT=ones[:], rhs=gain_rows[:], start=True, stop=True)
            banks["gains"] = gb

        def gain_tables():
            gb = banks["gains"]
            for j in range(2):
                nc.vector.tensor_copy(out=gain_cos[:, :, j, :], in_=gb[:, 0 : 2 * HD].rearrange("p (q d) -> p q d", q=2))
            for j in range(2):
                first = gain_cos[:, :, j, 0:32].rearrange("p q (h i) -> p q h i", h=2)
                nc.gpsimd.tensor_tensor(
                    out=gain_sin[:, :, j, :].rearrange("p q (h i) -> p q h i", h=2),
                    in0=first,
                    in1=trig[:, j, 0:3:2, :].unsqueeze(1).to_broadcast([P, 2, 2, 16]),
                    op=ALU.mult,
                )
                nc.gpsimd.tensor_tensor(
                    out=first, in0=first, in1=trig[:, j, 1:2, :].unsqueeze(1).to_broadcast([P, 2, 2, 16]), op=ALU.mult
                )

        units = list(HEAD)
        units.extend([(ci, g) for ci in range(2, 5) for g in range(PASSES)])
        n = len(units)
        last_step = {}
        for i in range(n):
            last_step[units[i][0]] = i
        last_step[VCH] = 0
        s_units = [u for u in units if u in T_UNITS or (u[0] != KCH and u not in V_WIDENS)]
        s_step = {}
        for k in range(len(s_units)):
            at = units.index(s_units[k])
            s_step[s_units[k]] = at - LOOK if k == 0 else max(at - LOOK_MAX, min(at - LOOK, s_step[s_units[k - 1]] + 1))
        windows = [0]
        bank_queue = {}
        for ci in range(6):
            for a in range(TT):
                bank_queue.setdefault(acc_bank(ci, a), []).append((ci, a))
        pending = []
        x_ready = []
        sq_todo = [(ci, a) for ci in range(5) for a in range(TT)]
        norm_todo = [(ci, a) for ci in range(5) for a in range(TT)]
        v_todo = [a for a in range(TT)]
        sq_done = []
        mm_left = {}
        for ci in range(6):
            for a in range(TT):
                mm_left[(ci, a)] = PASSES

        roots = []
        late = []
        tail = [False]
        to_empty = []
        to_il = []

        def do_roots():
            for group in roots:
                root(group)
                sq_done.append(group)
            roots.clear()

        def first_stage(i):
            for u in s_units:
                if s_step[u] == i:
                    if u[0] != KCH:
                        widen(u[0], u[1], do_roots)
                    if u in S_IL:
                        s_interleave(u[0], u[1])
                    if u in T_UNITS:
                        to_il.append(u)
            for e in list(to_empty):
                if units.index(e) - 1 <= i:
                    t_empty(e[0], e[1])
                    to_empty.remove(e)
            for u in list(to_il):
                if not to_empty:
                    t_interleave(u[0], u[1])
                    to_empty.append(u)
                    to_il.remove(u)
            do_roots()

        def second_stage(i):
            if i < n and units[i] not in T_UNITS and units[i] not in S_IL:
                interleave(units[i][0], units[i][1])

        def run_matmuls():
            for item in list(pending):
                ci, g, a = item
                b = acc_bank(ci, a)
                if a not in x_ready:
                    continue
                if (ci, a) not in banks:
                    if bank_user.get(b) is not None or bank_queue[b][0] != (ci, a) or (b >= 6 and staging_left[0] > 0):
                        continue
                    banks[(ci, a)] = bank(b)
                    bank_user[b] = (ci, a)
                    bank_queue[b].remove((ci, a))
                if any(p[0] == ci and p[2] == a and p[1] < g for p in pending):
                    continue
                multiply(ci, g, a)
                mm_left[(ci, a)] -= 1
                pending.remove(item)

        def take_x(a):
            for b in X_BANKS[a]:
                assert bank_user.get(b) is None
                bank_user[b] = ("x", a)
            x_transpose(a)

        def take(todo):
            item = todo[0]
            todo.remove(item)
            return item

        gain_matmul()
        bank_user[GAIN_BANK] = "gains"
        first = min(s_step[u] for u in s_units)
        for i in range(first, 0):
            first_stage(i)
        take_x(0)
        second_stage(0)

        for i in range(n + 12):
            group = []
            while sq_todo and len(group) < RATE and mm_left[sq_todo[0]] == 0 and i >= last_step[sq_todo[0][0]] + D_SQ[sq_todo[0][0]]:
                group.append(take(sq_todo))
            if group:
                squares(group)
                roots.append(group)
            first_stage(i)
            if i == SIN_STEP:
                sines()
            if i in X_COPY:
                a = X_COPY.index(i)
                if a + 1 < TT:
                    take_x(a + 1)
                x_copy(a)
                for b in X_BANKS[a]:
                    bank_user[b] = None
            if i == GAIN_STEP:
                gain_tables()
                bank_user[GAIN_BANK] = None
            now = []
            if sq_done and i >= last_step[sq_done[0][0][0]] + D_NORM[sq_done[0][0][0]]:
                now = take(sq_done)
                for item in now:
                    norm_todo.remove(item)
            if i + 2 < n and units[i + 2] in V_WIDENS:
                widen_v(units[i + 2][0], units[i + 2][1])
            second_stage(i + 1)
            if windows[0] == 2 * PASSES:
                g_quantize(2 * PASSES - 1)
                windows[0] += 1
            if now:
                if 0 < windows[0] < 2 * PASSES:
                    g_quantize(windows[0] - 1)
                if windows[0] < 2 * PASSES:
                    g_interleave(windows[0])
                    windows[0] += 1
            if now:
                norm_b(now)
            for ci, a in now:
                bank_user[acc_bank(ci, a)] = None
            if i < n:
                quantize(units[i][0], units[i][1])
                for a in range(TT):
                    pending.append((units[i][0], units[i][1], a))
            if i in X_QUANT:
                x_quantize(X_QUANT.index(i))
                x_ready.append(X_QUANT.index(i))
            tail[0] = i >= n
            if now and (i < n or not LATE_SUMS):
                norm_c(now)
            elif now:
                late.append(now)
                if len(late) > 1 or not norm_todo:
                    norm_c(take(late))
                if late and not norm_todo:
                    norm_c(take(late))
            run_matmuls()
            for a in list(v_todo):
                if mm_left[(VCH, a)] == 0 and not sq_todo and not roots:
                    value_out(a)
                    v_todo.remove(a)
        assert not pending and not norm_todo and not sq_todo and not v_todo and not to_empty
